import numpy as np
import ml_dtypes


def mxq(x, axis, fmt="e4m3"):
    dtype, down = {"e4m3": (ml_dtypes.float8_e4m3fn, 7), "e5m2": (ml_dtypes.float8_e5m2, 14)}[fmt]
    v = np.moveaxis(np.asarray(x, np.float32).astype(ml_dtypes.bfloat16).astype(np.float64), axis, -1)
    blocks = v.reshape(v.shape[:-1] + (-1, 32))
    amax = np.abs(blocks).max(-1, keepdims=True)
    byte = np.maximum(np.where(amax > 0, np.frexp(amax)[1] - 1 + 127, 0) - down, 1)
    scale = np.exp2(byte - 127.0)
    codes = (blocks / scale).astype(np.float32).astype(dtype).astype(np.float64)
    return np.moveaxis((codes * scale).reshape(v.shape), -1, axis)


WIDE = False


def mx_kscale(k):
    if not WIDE:
        return np.ones(k)
    levels = np.array([10, -10, 5, -5, 0])
    a = np.random.permutation(np.resize(levels, k // 512 * 4)).reshape(k // 512, 4)
    idx = np.arange(k)
    return np.exp2(a[idx // 512, idx % 128 // 32])


BF16 = ml_dtypes.bfloat16


def bf(x):
    return np.asarray(x, np.float32).astype(BF16)


def f64(x):
    return np.asarray(x).astype(np.float64)


E2M1 = np.array([0.0, 0.5, 1.0, 1.5, 2.0, 3.0, 4.0, 6.0, -0.0, -0.5, -1.0, -1.5, -2.0, -3.0, -4.0, -6.0])


def pack_weight(w, fmt):
    k, n = w.shape
    w = f64(bf(w)).reshape(k // 32, 32, n)
    amax = np.abs(w).max(1)
    if fmt == "e4m3":
        byte = np.frexp(amax)[1] - 1 + 127 - 7
    else:
        mant, ex = np.frexp(amax / 6.0)
        byte = np.where(mant > 0.5, ex, ex - 1) + 127
    byte = np.clip(np.where(amax > 0, byte, 1), 1, 254)
    scaled = (w * np.exp2(127.0 - byte)[:, None, :]).reshape(k, n).astype(np.float32)
    by_word = np.ascontiguousarray(scaled.reshape(k // 512, 128, 4, n).transpose(0, 1, 3, 2))
    if fmt == "e4m3":
        words = by_word.astype(ml_dtypes.float8_e4m3fn).view(np.uint8)
    else:
        c = by_word.astype(ml_dtypes.float4_e2m1fn).view(np.uint8) & 0xF
        words = c[..., 0::2] | (c[..., 1::2] << 4)
    return np.ascontiguousarray(words), np.ascontiguousarray(byte.astype(np.uint8).reshape(k // 512, 16, n))


def unpack_weight(words, scales, fmt):
    g, p, n, _ = words.shape
    if fmt == "e4m3":
        vals = np.ascontiguousarray(words).view(ml_dtypes.float8_e4m3fn).astype(np.float64)
    else:
        nib = np.empty((g, p, n, 4), np.uint8)
        nib[..., 0::2] = words & 0xF
        nib[..., 1::2] = words >> 4
        vals = E2M1[nib]
    vals = vals * np.repeat(np.exp2(scales.astype(np.float64) - 127.0), 8, axis=1)[..., None]
    return vals.transpose(0, 1, 3, 2).reshape(g * 512, n)


B, C, H, W, KERNEL, M, O = 128, 1, 34, 66, 3, 2048, 256
K = C * KERNEL * KERNEL
HO, WO = H - KERNEL + 1, W - KERNEL + 1
L = HO * WO


def unfold(x):
    cols = [x[:, :, i:i + HO, j:j + WO] for i in range(KERNEL) for j in range(KERNEL)]
    return np.stack(cols, axis=2).reshape(B, K, L)


def setup_inputs():
    t = mx_kscale(K * M)[:M]
    x = bf(np.random.standard_normal((B, C, H, W)))
    G_words, G_scales = pack_weight((np.random.standard_normal((M, L)) / np.sqrt(L) * t[:, None]).T, "e4m3")
    v = bf(np.random.standard_normal((M, K, O)) * 0.7 / np.sqrt(K * M) / t[:, None, None])
    w = bf(np.random.standard_normal((M, K, O)) * 0.7 / np.sqrt(K * M) / t[:, None, None])
    return {"x": x, "G_words": G_words, "G_scales": G_scales, "v": v, "w": w}


def reference(x, G_words, G_scales, v, w):
    U = unfold(f64(x))
    A = mxq(U, 2, "e4m3") @ unpack_weight(G_words, G_scales, "e4m3")
    p_diff = f64(v) - f64(w)
    return mxq(A.reshape(B, K * M), 1, "e4m3") @ mxq(p_diff.transpose(1, 0, 2).reshape(K * M, O), 0, "e4m3")

@@ -1,0 +1,216 @@
+from contextlib import ExitStack
+
+import concourse.mybir as mybir
+from concourse.masks import make_identity
+
+F32 = mybir.dt.float32
+BF16 = mybir.dt.bfloat16
+I32 = mybir.dt.int32
+U32 = mybir.dt.uint32
+U8 = mybir.dt.uint8
+FP8X4 = mybir.dt.float8_e4m3fn_x4
+
+P = 128
+B = 128
+H = 34
+W = 66
+HO = 32
+WO = 64
+KK = 9
+M = 2048
+O = 256
+NG = 4
+MG = 4
+FLOPS = 2 * B * KK * M * (HO * WO) + 2 * B * KK * M * O
+
+PIECES = (
+    (0, 4, ((0, 3, "s"), (3, 1, "v"))),
+    (4, 4, ((4, 2, "s"), (6, 2, "v"))),
+    (8, 1, ((8, 1, "v"),)),
+)
+
+
+def tile_convexrelucnn_w_kernel(tc, x, G_words, G_scales, v, w, out):
+    nc = tc.nc
+    with ExitStack() as ctx:
+        keep = ctx.enter_context(tc.tile_pool(name="keep", bufs=1))
+        stream = ctx.enter_context(tc.tile_pool(name="stream", bufs=2))
+        psum = ctx.enter_context(tc.psum_pool(name="psum", bufs=7))
+        psum_out = ctx.enter_context(tc.psum_pool(name="psum_out", bufs=1))
+
+        x_sb = keep.tile([P, H * W], BF16, align_bytes=64)
+        nc.sync.dma_start(out=x_sb[:], in_=x.rearrange("b c h w -> b (c h w)"))
+
+        w_planes = keep.tile([P, M], U8, align_bytes=64)
+        nc.vector.memset(w_planes[:].bitcast(I32), 0)
+        for q in range(4):
+            nc.sync.dma_start(
+                out=w_planes[32 * q : 32 * q + 16, :].bitcast(I32),
+                in_=G_scales[:, 4 * q : 4 * q + 4, :].bitcast(I32),
+            )
+
+        ident = keep.tile([P, P], F32)
+        make_identity(nc, ident[:])
+
+        g_bytes = G_words.rearrange("g p m t -> p g (m t)")
+        w_codes = []
+
+        def load_w_codes(gp):
+            wc = keep.tile([P, NG, 512], U32, name="wc%d" % gp, align_bytes=64)
+            nc.sync.dma_start(
+                out=wc[:].bitcast(I32),
+                in_=g_bytes[:, :, 2048 * gp : 2048 * (gp + 1)].bitcast(I32),
+            )
+            w_codes.append(wc)
+
+        v_tiles = {}
+        w_tiles = {}
+
+        def load_vw(gp):
+            vt = stream.tile([P, 4, KK * O], BF16, name="vt", tag="vt", bufs=2)
+            v_tiles[gp] = vt
+            for t in range(4):
+                m0 = 512 * gp + 128 * t
+                nc.sync.dma_start(out=vt[:, t, :], in_=v[m0 : m0 + 128].rearrange("p k o -> p (k o)"))
+                wt = stream.tile([P, KK * O], BF16, name="wt", tag="wt", bufs=4)
+                nc.sync.dma_start(out=wt[:], in_=w[m0 : m0 + 128].rearrange("p k o -> p (k o)"))
+                w_tiles[(gp, t)] = wt
+
+        load_w_codes(0)
+        load_w_codes(1)
+        load_vw(0)
+        load_w_codes(2)
+
+        xs = keep.tile([P, 3, 2, H * 16], F32)
+        xw = x_sb[:].bitcast(F32).rearrange("b (r c) -> b r c", c=W // 2)
+        xb = x_sb[:].rearrange("b (r c) -> b r c", c=W)
+        nc.vector.tensor_copy(
+            out=xs[:, 0].rearrange("b u (r c) -> b u r c", c=16),
+            in_=xw[:, :, 0:32].rearrange("b r (c u) -> b u r c", u=2),
+        )
+        nc.scalar.copy(
+            out=xs[:, 2].rearrange("b u (r c) -> b u r c", c=16),
+            in_=xw[:, :, 1:33].rearrange("b r (c u) -> b u r c", u=2),
+        )
+        odd = xb[:, :, 1:65].rearrange("b r (c u e) -> b u r c e", u=2, e=2)
+        nc.vector.tensor_copy(
+            out=xs[:, 1, 0, :].bitcast(BF16).rearrange("b (r c e) -> b r c e", c=16, e=2),
+            in_=odd[:, 0],
+        )
+        nc.scalar.copy(
+            out=xs[:, 1, 1, :].bitcast(BF16).rearrange("b (r c e) -> b r c e", c=16, e=2),
+            in_=odd[:, 1],
+        )
+
+        u_codes = keep.tile([P, KK, 512], U32, align_bytes=64)
+        u_planes = keep.tile([P, KK, 512], U8, align_bytes=64)
+        for k in (0, 3, 6, 2, 5, 8, 1, 4, 7):
+            i, j = divmod(k, 3)
+            su = stream.tile([P, 2048], BF16, name="su", tag="stg", bufs=3, align_bytes=64)
+            su_words = su[:].bitcast(F32).rearrange("p (g b u) -> p g b u", g=NG, u=2)
+            for h in range(2):
+                pt = psum.tile([P, 2, 2, P], F32, name="pt", tag="bank")
+                for s in range(2):
+                    g = 2 * h + s
+                    c0 = (8 * g + i) * 16
+                    for u in range(2):
+                        nc.tensor.transpose(pt[:, s, u, :], xs[:, j, u, c0 : c0 + P], ident[:])
+                src = pt[:].rearrange("p s u b -> p s b u")
+                if h == 0:
+                    nc.vector.tensor_copy(out=su_words[:, 0:2], in_=src)
+                else:
+                    nc.scalar.copy(out=su_words[:, 2:4], in_=src)
+            nc.vector.quantize_mx(
+                out=u_codes[:, k, :].bitcast(FP8X4), scales=u_planes[:, k, :], in_=su[:]
+            )
+
+        a_codes = keep.tile([P, MG * KK * P], U32, align_bytes=64)
+        a_planes = keep.tile([P, MG * KK * P], U8, align_bytes=64)
+        p_codes = keep.tile([P, MG * KK * O], U32, align_bytes=64)
+        p_planes = keep.tile([P, MG * KK * O], U8, align_bytes=64)
+        acc = psum_out.tile([P, O], F32)
+
+        ag_now = [None]
+
+        def first_matmul(gp, k):
+            s = gp * KK + k
+            bank = psum.tile([P, 4, P], F32, name="bank", tag="bank")
+            for t in range(4):
+                m0 = 512 * gp + 128 * t
+                for g in range(NG):
+                    nc.tensor.matmul_mx(
+                        out=bank[:, t, :],
+                        lhsT=w_codes[gp][:, g, 128 * t : 128 * (t + 1)].bitcast(FP8X4),
+                        lhsT_scale=w_planes[4 * g : P, m0 : m0 + 128],
+                        rhs=u_codes[:, k, 128 * g : 128 * (g + 1)].bitcast(FP8X4),
+                        rhs_scale=u_planes[:, k, 128 * g : 128 * (g + 1)],
+                        start=(g == 0),
+                        stop=(g == NG - 1),
+                    )
+            if s % 4 == 0:
+                ag_now[0] = stream.tile([P, 4, P, 4], BF16, name="ag", tag="ag", bufs=2, align_bytes=64)
+            ag = ag_now[0]
+            nc.scalar.copy(out=ag[:, s % 4], in_=bank[:].rearrange("p t b -> p b t"))
+            if s % 4 == 3:
+                c0 = (s - 3) * P
+                nc.vector.quantize_mx(
+                    out=a_codes[:, c0 : c0 + 512].bitcast(FP8X4),
+                    scales=a_planes[:, c0 : c0 + 512],
+                    in_=ag[:].rearrange("p s b t -> p (s b t)"),
+                )
+
+        def p_piece(gp, piece):
+            k0, nk, shares = piece
+            vt = v_tiles[gp]
+            pg = stream.tile([P, 4096], BF16, name="pg", tag="stg", bufs=3, align_bytes=64)
+            for ks, n, eng in shares:
+                dst = pg[:, (ks - k0) * 1024 : (ks - k0 + n) * 1024].rearrange(
+                    "p (c i t) -> p c t i", i=4, t=4
+                )
+                src = vt[:, :, ks * O : (ks + n) * O].rearrange("p t (c i) -> p c t i", i=4)
+                if eng == "s":
+                    nc.scalar.copy(out=dst, in_=src)
+                else:
+                    nc.vector.tensor_copy(out=dst, in_=src)
+            c0 = (gp * KK + k0) * O
+            nc.vector.quantize_mx(
+                out=p_codes[:, c0 : c0 + nk * O].bitcast(FP8X4),
+                scales=p_planes[:, c0 : c0 + nk * O],
+                in_=pg[:, 0 : nk * 1024],
+            )
+
+        def second_matmul(gp):
+            for k in range(KK):
+                s = gp * KK + k
+                nc.tensor.matmul_mx(
+                    out=acc[:],
+                    lhsT=a_codes[:, s * P : (s + 1) * P].bitcast(FP8X4),
+                    lhsT_scale=a_planes[:, s * P : (s + 1) * P],
+                    rhs=p_codes[:, s * O : (s + 1) * O].bitcast(FP8X4),
+                    rhs_scale=p_planes[:, s * O : (s + 1) * O],
+                    start=(s == 0),
+                    stop=(s == MG * KK - 1),
+                )
+
+        for gp in range(MG):
+            for t in range(4):
+                vt = v_tiles[gp]
+                nc.vector.tensor_tensor(
+                    out=vt[:, t, :], in0=vt[:, t, :], in1=w_tiles[(gp, t)][:],
+                    op=mybir.AluOpType.subtract,
+                )
+            if gp + 1 < MG:
+                load_vw(gp + 1)
+            if gp == 0:
+                load_w_codes(3)
+            for k in range(KK):
+                first_matmul(gp, k)
+                if k in (2, 5, 7):
+                    p_piece(gp, PIECES[(2, 5, 7).index(k)])
+                if gp > 0 and k == 3:
+                    second_matmul(gp - 1)
+        second_matmul(MG - 1)
+
+        res = keep.tile([P, O], F32)
+        nc.vector.tensor_copy(out=res[:], in_=acc[:])
+        nc.sync.dma_start(out=out, in_=res[:])

@@ -14,203 +14,302 @@ P = 128
 B = 128
 H = 34
 W = 66
-HO = 32
-WO = 64
 KK = 9
 M = 2048
 O = 256
 NG = 4
 MG = 4
-FLOPS = 2 * B * KK * M * (HO * WO) + 2 * B * KK * M * O
+NR = MG * KK
+FLOPS = 2 * B * KK * M * 2048 + 2 * B * KK * M * O
 
-PIECES = (
-    (0, 4, ((0, 3, "s"), (3, 1, "v"))),
-    (4, 4, ((4, 2, "s"), (6, 2, "v"))),
-    (8, 1, ((8, 1, "v"),)),
+PIN = False
+CHUNKS = (
+    (0, 0, 2, -3, (0, 1), (1, 1), ((0, 2),)),
+    (0, 2, 3, -1, (2, 2), (4, 1), ((2, 2), (4, 1))),
+    (0, 5, 4, 3, (5, 3), (8, 1), ((5, 4),)),
+    (1, 0, 5, 8, (0, 3), (3, 2), ((0, 4), (4, 1))),
+    (1, 5, 4, 13, (5, 3), (8, 1), ((5, 4),)),
+    (2, 0, 5, 17, (0, 3), (3, 2), ((0, 4), (4, 1))),
+    (2, 5, 4, 22, (5, 3), (8, 1), ((5, 4),)),
+    (3, 0, 5, 26, (0, 3), (3, 2), ((0, 4), (4, 1))),
+    (3, 5, 2, 31, (5, 1), (6, 1), ((5, 2),)),
+    (3, 7, 2, 33, (7, 1), (8, 1), ((7, 2),)),
 )
+A_CALLS = ((0, 4), (4, 4), (8, 4), (12, 4), (16, 4), (20, 4), (24, 4), (28, 4), (32, 2), (34, 1), (35, 1))
+K_ORDER = (0, 3, 6, 2, 5, 8, 1, 4, 7)
+PLANE = ((0, 1), (3, 4), (1, 2))
+LOAD_SEQ = (("c", 0), ("w", 0), ("c", 1), ("c", 2), ("w", 1), ("c", 3), ("c", 4), ("w", 2), ("c", 5), ("c", 6), ("w", 3), ("c", 7), ("c", 8), ("c", 9))
+PRELOAD = 2
+MAXK = 5
+NV = 4
+NW = 3
+NSTG = 3
+QLAG = 4
+PASS_LAG = 1
 
 
 def tile_convexrelucnn_w_kernel(tc, x, G_words, G_scales, v, w, out):
     nc = tc.nc
     with ExitStack() as ctx:
+        if PIN:
+            ctx.enter_context(tc.manual_schedule())
         keep = ctx.enter_context(tc.tile_pool(name="keep", bufs=1))
         stream = ctx.enter_context(tc.tile_pool(name="stream", bufs=2))
         psum = ctx.enter_context(tc.psum_pool(name="psum", bufs=7))
         psum_out = ctx.enter_context(tc.psum_pool(name="psum_out", bufs=1))
 
-        x_sb = keep.tile([P, H * W], BF16, align_bytes=64)
-        nc.sync.dma_start(out=x_sb[:], in_=x.rearrange("b c h w -> b (c h w)"))
-
         w_planes = keep.tile([P, M], U8, align_bytes=64)
-        nc.vector.memset(w_planes[:].bitcast(I32), 0)
-        for q in range(4):
-            nc.sync.dma_start(
-                out=w_planes[32 * q : 32 * q + 16, :].bitcast(I32),
-                in_=G_scales[:, 4 * q : 4 * q + 4, :].bitcast(I32),
-            )
+        u_codes = keep.tile([P, 24 * P], U32, align_bytes=64)
+        u_planes = keep.tile([P, 24 * P], U8, align_bytes=64)
+        p_codes = keep.tile([P, NR * O], U32, align_bytes=64)
+        p_planes = keep.tile([P, NR * O], U8, align_bytes=64)
+        res = keep.tile([P, O], F32)
+        acc = psum_out.tile([P, O], F32)
 
-        ident = keep.tile([P, P], F32)
-        make_identity(nc, ident[:])
-
-        g_bytes = G_words.rearrange("g p m t -> p g (m t)")
-        w_codes = []
-
-        def load_w_codes(gp):
-            wc = keep.tile([P, NG, 512], U32, name="wc%d" % gp, align_bytes=64)
-            nc.sync.dma_start(
-                out=wc[:].bitcast(I32),
-                in_=g_bytes[:, :, 2048 * gp : 2048 * (gp + 1)].bitcast(I32),
-            )
-            w_codes.append(wc)
-
+        g_rows = G_words.rearrange("g p m t -> (g p) (m t)").rearrange(
+            "(s q r) x -> q s r x", q=NG, r=8
+        )
+        w_codes = {}
         v_tiles = {}
         w_tiles = {}
 
-        def load_vw(gp):
-            vt = stream.tile([P, 4, KK * O], BF16, name="vt", tag="vt", bufs=2)
-            v_tiles[gp] = vt
-            for t in range(4):
-                m0 = 512 * gp + 128 * t
-                nc.sync.dma_start(out=vt[:, t, :], in_=v[m0 : m0 + 128].rearrange("p k o -> p (k o)"))
-                wt = stream.tile([P, KK * O], BF16, name="wt", tag="wt", bufs=4)
-                nc.sync.dma_start(out=wt[:], in_=w[m0 : m0 + 128].rearrange("p k o -> p (k o)"))
-                w_tiles[(gp, t)] = wt
+        def load_w_codes(gp):
+            wc = keep.tile([P, NG, 512], U32, name="wc%d" % gp, align_bytes=64)
+            for q in range(NG):
+                nc.sync.dma_start(
+                    out=wc[:, q, :].bitcast(I32),
+                    in_=g_rows[q][:, :, 2048 * gp : 2048 * (gp + 1)].bitcast(I32),
+                )
+            w_codes[gp] = wc
 
-        load_w_codes(0)
-        load_w_codes(1)
-        load_vw(0)
-        load_w_codes(2)
+        def load_chunk(c):
+            gp, k0, nk = CHUNKS[c][0:3]
+            vc = stream.tile([P, 4, MAXK * O], BF16, name="vc", tag="vc", bufs=NV)
+            wn = stream.tile([P, 4, MAXK * O], BF16, name="wn", tag="wn", bufs=NW)
+            for dst, src in ((vc, v), (wn, w)):
+                nc.sync.dma_start(
+                    out=dst[:, :, 0 : nk * O],
+                    in_=src[512 * gp : 512 * (gp + 1), k0 : k0 + nk, :].rearrange(
+                        "(t p) k o -> p t (k o)", p=P
+                    ),
+                )
+            v_tiles[c] = vc
+            w_tiles[c] = wn
 
-        xs = keep.tile([P, 3, 2, H * 16], F32)
-        xw = x_sb[:].bitcast(F32).rearrange("b (r c) -> b r c", c=W // 2)
-        xb = x_sb[:].rearrange("b (r c) -> b r c", c=W)
-        nc.vector.tensor_copy(
-            out=xs[:, 0].rearrange("b u (r c) -> b u r c", c=16),
-            in_=xw[:, :, 0:32].rearrange("b r (c u) -> b u r c", u=2),
-        )
-        nc.scalar.copy(
-            out=xs[:, 2].rearrange("b u (r c) -> b u r c", c=16),
-            in_=xw[:, :, 1:33].rearrange("b r (c u) -> b u r c", u=2),
-        )
-        odd = xb[:, :, 1:65].rearrange("b r (c u e) -> b u r c e", u=2, e=2)
-        nc.vector.tensor_copy(
-            out=xs[:, 1, 0, :].bitcast(BF16).rearrange("b (r c e) -> b r c e", c=16, e=2),
-            in_=odd[:, 0],
-        )
-        nc.scalar.copy(
-            out=xs[:, 1, 1, :].bitcast(BF16).rearrange("b (r c e) -> b r c e", c=16, e=2),
-            in_=odd[:, 1],
-        )
+        load_pos = [0]
 
-        u_codes = keep.tile([P, KK, 512], U32, align_bytes=64)
-        u_planes = keep.tile([P, KK, 512], U8, align_bytes=64)
-        for k in (0, 3, 6, 2, 5, 8, 1, 4, 7):
-            i, j = divmod(k, 3)
-            su = stream.tile([P, 2048], BF16, name="su", tag="stg", bufs=3, align_bytes=64)
-            su_words = su[:].bitcast(F32).rearrange("p (g b u) -> p g b u", g=NG, u=2)
-            for h in range(2):
-                pt = psum.tile([P, 2, 2, P], F32, name="pt", tag="bank")
-                for s in range(2):
-                    g = 2 * h + s
-                    c0 = (8 * g + i) * 16
-                    for u in range(2):
-                        nc.tensor.transpose(pt[:, s, u, :], xs[:, j, u, c0 : c0 + P], ident[:])
-                src = pt[:].rearrange("p s u b -> p s b u")
-                if h == 0:
-                    nc.vector.tensor_copy(out=su_words[:, 0:2], in_=src)
+        def loads_through(c):
+            while load_pos[0] < len(LOAD_SEQ):
+                kind, n = LOAD_SEQ[load_pos[0]]
+                if kind == "c" and n > c:
+                    break
+                load_pos[0] += 1
+                if kind == "c":
+                    load_chunk(n)
                 else:
-                    nc.scalar.copy(out=su_words[:, 2:4], in_=src)
-            nc.vector.quantize_mx(
-                out=u_codes[:, k, :].bitcast(FP8X4), scales=u_planes[:, k, :], in_=su[:]
+                    load_w_codes(n)
+
+        with tc.tile_pool(name="early", bufs=1) as early:
+            x_sb = early.tile([P, H * W], BF16, align_bytes=64)
+            nc.sync.dma_start(out=x_sb[:], in_=x.rearrange("b c h w -> b (c h w)"))
+            nc.vector.memset(w_planes[:].bitcast(I32), 0)
+            s_rows = G_scales.rearrange("g q m -> (g q) m").rearrange(
+                "(a r q) m -> a q r m", r=4, q=NG
             )
+            for a in range(4):
+                nc.sync.dma_start(
+                    out=w_planes[32 * a : 32 * a + 16, :].bitcast(I32),
+                    in_=s_rows[a].bitcast(I32),
+                )
+            ident = early.tile([P, P], F32)
+            make_identity(nc, ident[:])
+            loads_through(PRELOAD)
 
-        a_codes = keep.tile([P, MG * KK * P], U32, align_bytes=64)
-        a_planes = keep.tile([P, MG * KK * P], U8, align_bytes=64)
-        p_codes = keep.tile([P, MG * KK * O], U32, align_bytes=64)
-        p_planes = keep.tile([P, MG * KK * O], U8, align_bytes=64)
-        acc = psum_out.tile([P, O], F32)
+            xs = early.tile([P, 5, 2, 2, 17 * 8], F32)
+            xw = x_sb[:].bitcast(F32).rearrange("b (r c) -> b r c", c=W // 2)
+            xb = x_sb[:].rearrange("b (r c) -> b r c", c=W)
+            even0 = xw[:, :, 0:32].rearrange("b (r a) (h c u) -> b u a h r c", a=2, h=2, u=2)
+            even2 = xw[:, :, 1:33].rearrange("b (r a) (h c u) -> b u a h r c", a=2, h=2, u=2)
+            odd = xb[:, :, 1:65].rearrange("b (r a) (h c u e) -> b u a h r c e", a=2, h=2, u=2, e=2)
+            for u in range(2):
+                nc.vector.tensor_copy(
+                    out=xs[:, u].rearrange("b a h (r c) -> b a h r c", c=8), in_=even0[:, u]
+                )
+            for par in range(2):
+                nc.scalar.copy(
+                    out=xs[:, 2, par].rearrange("b h (r c) -> b h r c", c=8), in_=even2[:, 1, par]
+                )
+            for par in range(2):
+                nc.vector.tensor_copy(
+                    out=xs[:, 3, par].bitcast(BF16).rearrange("b h (r c e) -> b h r c e", c=8, e=2),
+                    in_=odd[:, 0, par],
+                )
+                for h in range(2):
+                    nc.scalar.copy(
+                        out=xs[:, 4, par, h].bitcast(BF16).rearrange("b (r c e) -> b r c e", c=8, e=2),
+                        in_=odd[:, 1, par, h],
+                    )
 
-        ag_now = [None]
+            n_bank = 0
+            for j in (0, 2, 1):
+                su = stream.tile([P, 4096], BF16, name="su", tag="stg", bufs=NSTG, align_bytes=64)
+                su_words = su[:].bitcast(F32).rearrange("p (g b u) -> p g b u", g=8, u=2)
+                for rho in range(4):
+                    pt = psum.tile([P, 2, 2, P], F32, name="pt", tag="bank")
+                    for h in range(2):
+                        c0 = 8 * (rho // 2)
+                        for u in range(2):
+                            nc.tensor.transpose(
+                                pt[:, h, u, :], xs[:, PLANE[j][u], rho % 2, h, c0 : c0 + P], ident[:]
+                            )
+                    src = pt[:].rearrange("p s u b -> p s b u")
+                    if n_bank % 4 == 0:
+                        nc.vector.tensor_copy(out=su_words[:, 2 * rho : 2 * rho + 2], in_=src)
+                    else:
+                        nc.scalar.copy(out=su_words[:, 2 * rho : 2 * rho + 2], in_=src)
+                    n_bank += 1
+                nc.vector.quantize_mx(
+                    out=u_codes[:, j * 1024 : (j + 1) * 1024].bitcast(FP8X4),
+                    scales=u_planes[:, j * 1024 : (j + 1) * 1024],
+                    in_=su[:],
+                )
 
-        def first_matmul(gp, k):
-            s = gp * KK + k
+        late = ctx.enter_context(tc.tile_pool(name="late", bufs=1))
+        a_codes = late.tile([P, NR * P], U32, align_bytes=64)
+        a_planes = late.tile([P, NR * P], U8, align_bytes=64)
+
+        banks = {}
+        a_stage = {}
+        call_of = {}
+        for first, n in A_CALLS:
+            for s in range(first, first + n):
+                call_of[s] = (first, n)
+
+        def first_matmul(s):
+            gp, n = divmod(s, KK)
+            i, j = divmod(K_ORDER[n], 3)
             bank = psum.tile([P, 4, P], F32, name="bank", tag="bank")
             for t in range(4):
                 m0 = 512 * gp + 128 * t
                 for g in range(NG):
+                    u0 = (8 * j + 2 * (g // 2 + i) + g % 2) * P
                     nc.tensor.matmul_mx(
                         out=bank[:, t, :],
                         lhsT=w_codes[gp][:, g, 128 * t : 128 * (t + 1)].bitcast(FP8X4),
                         lhsT_scale=w_planes[4 * g : P, m0 : m0 + 128],
-                        rhs=u_codes[:, k, 128 * g : 128 * (g + 1)].bitcast(FP8X4),
-                        rhs_scale=u_planes[:, k, 128 * g : 128 * (g + 1)],
+                        rhs=u_codes[:, u0 : u0 + P].bitcast(FP8X4),
+                        rhs_scale=u_planes[:, u0 : u0 + P],
                         start=(g == 0),
                         stop=(g == NG - 1),
                     )
-            if s % 4 == 0:
-                ag_now[0] = stream.tile([P, 4, P, 4], BF16, name="ag", tag="ag", bufs=2, align_bytes=64)
-            ag = ag_now[0]
-            nc.scalar.copy(out=ag[:, s % 4], in_=bank[:].rearrange("p t b -> p b t"))
-            if s % 4 == 3:
-                c0 = (s - 3) * P
-                nc.vector.quantize_mx(
-                    out=a_codes[:, c0 : c0 + 512].bitcast(FP8X4),
-                    scales=a_planes[:, c0 : c0 + 512],
-                    in_=ag[:].rearrange("p s b t -> p (s b t)"),
-                )
+            banks[s] = bank
 
-        def p_piece(gp, piece):
-            k0, nk, shares = piece
-            vt = v_tiles[gp]
-            pg = stream.tile([P, 4096], BF16, name="pg", tag="stg", bufs=3, align_bytes=64)
-            for ks, n, eng in shares:
-                dst = pg[:, (ks - k0) * 1024 : (ks - k0 + n) * 1024].rearrange(
-                    "p (c i t) -> p c t i", i=4, t=4
+        def leave_psum(s):
+            first, n = call_of[s]
+            if s == first:
+                a_stage[first] = stream.tile(
+                    [P, 4, P, 4], BF16, name="ag", tag="ag", bufs=3, align_bytes=64
                 )
-                src = vt[:, :, ks * O : (ks + n) * O].rearrange("p t (c i) -> p c t i", i=4)
-                if eng == "s":
-                    nc.scalar.copy(out=dst, in_=src)
-                else:
-                    nc.vector.tensor_copy(out=dst, in_=src)
-            c0 = (gp * KK + k0) * O
-            nc.vector.quantize_mx(
-                out=p_codes[:, c0 : c0 + nk * O].bitcast(FP8X4),
-                scales=p_planes[:, c0 : c0 + nk * O],
-                in_=pg[:, 0 : nk * 1024],
+            nc.scalar.copy(
+                out=a_stage[first][:, s - first], in_=banks[s][:].rearrange("p t b -> p b t")
             )
 
-        def second_matmul(gp):
-            for k in range(KK):
-                s = gp * KK + k
-                nc.tensor.matmul_mx(
-                    out=acc[:],
-                    lhsT=a_codes[:, s * P : (s + 1) * P].bitcast(FP8X4),
-                    lhsT_scale=a_planes[:, s * P : (s + 1) * P],
-                    rhs=p_codes[:, s * O : (s + 1) * O].bitcast(FP8X4),
-                    rhs_scale=p_planes[:, s * O : (s + 1) * O],
-                    start=(s == 0),
-                    stop=(s == MG * KK - 1),
-                )
+        def quantise_a(first, n):
+            nc.vector.quantize_mx(
+                out=a_codes[:, first * P : (first + n) * P].bitcast(FP8X4),
+                scales=a_planes[:, first * P : (first + n) * P],
+                in_=a_stage[first][:, 0:n].rearrange("p s b t -> p (s b t)"),
+            )
 
-        for gp in range(MG):
-            for t in range(4):
-                vt = v_tiles[gp]
-                nc.vector.tensor_tensor(
-                    out=vt[:, t, :], in0=vt[:, t, :], in1=w_tiles[(gp, t)][:],
-                    op=mybir.AluOpType.subtract,
-                )
-            if gp + 1 < MG:
-                load_vw(gp + 1)
-            if gp == 0:
-                load_w_codes(3)
-            for k in range(KK):
-                first_matmul(gp, k)
-                if k in (2, 5, 7):
-                    p_piece(gp, PIECES[(2, 5, 7).index(k)])
-                if gp > 0 and k == 3:
-                    second_matmul(gp - 1)
-        second_matmul(MG - 1)
+        p_stage = {}
 
-        res = keep.tile([P, O], F32)
+        def subtract(c):
+            nk = CHUNKS[c][2]
+            nc.vector.tensor_tensor(
+                out=v_tiles[c][:, :, 0 : nk * O],
+                in0=v_tiles[c][:, :, 0 : nk * O],
+                in1=w_tiles[c][:, :, 0 : nk * O],
+                op=mybir.AluOpType.subtract,
+            )
+            p_stage[c] = stream.tile(
+                [P, MAXK * 1024], BF16, name="pg", tag="stg", bufs=NSTG, align_bytes=64
+            )
+
+        def regroup(c, first, n, copy):
+            lo = first - CHUNKS[c][1]
+            copy(
+                out=p_stage[c][:, lo * 1024 : (lo + n) * 1024].rearrange(
+                    "p (c i t) -> p c t i", i=4, t=4
+                ),
+                in_=v_tiles[c][:, :, lo * O : (lo + n) * O].rearrange("p t (c i) -> p c t i", i=4),
+            )
+
+        def quantise_p(c, first, n):
+            gp, k0 = CHUNKS[c][0:2]
+            c0 = (gp * KK + first) * O
+            nc.vector.quantize_mx(
+                out=p_codes[:, c0 : c0 + n * O].bitcast(FP8X4),
+                scales=p_planes[:, c0 : c0 + n * O],
+                in_=p_stage[c][:, (first - k0) * 1024 : (first - k0 + n) * 1024],
+            )
+
+        passes_done = [0]
+
+        def second_matmul(s):
+            ra = (s // KK) * KK + K_ORDER.index(s % KK)
+            nc.tensor.matmul_mx(
+                out=acc[:],
+                lhsT=a_codes[:, ra * P : (ra + 1) * P].bitcast(FP8X4),
+                lhsT_scale=a_planes[:, ra * P : (ra + 1) * P],
+                rhs=p_codes[:, s * O : (s + 1) * O].bitcast(FP8X4),
+                rhs_scale=p_planes[:, s * O : (s + 1) * O],
+                start=(passes_done[0] == 0),
+                stop=(passes_done[0] == NR - 1),
+            )
+            passes_done[0] += 1
+
+        a_round = {}
+        for first, n in A_CALLS:
+            lag = 2 if first + n < NR - 3 else 1
+            for s in range(first, first + n):
+                a_round[s] = first + n - 1 + lag
+        p_round = {}
+        for gp, k0, nk, rho, s_part, v_part, calls in CHUNKS:
+            for k in range(k0, k0 + nk):
+                p_round[gp * KK + k] = rho + QLAG
+        ready = {}
+        for s in range(NR):
+            ready[s] = max(a_round[(s // KK) * KK + K_ORDER.index(s % KK)], p_round[s])
+            if ready[s] < NR - 3:
+                ready[s] += PASS_LAG
+        first_round = min(c[3] for c in CHUNKS)
+        last_round = max(ready[s] for s in range(NR))
+
+        for r in range(min(first_round, 0), last_round + 1):
+            if 0 <= r < NR:
+                first_matmul(r)
+            for c, (gp, k0, nk, rho, s_part, v_part, calls) in enumerate(CHUNKS):
+                if rho + 1 == r and s_part[1] > 0:
+                    regroup(c, s_part[0], s_part[1], nc.scalar.copy)
+            if 0 <= r < NR:
+                leave_psum(r)
+            for c, (gp, k0, nk, rho, s_part, v_part, calls) in enumerate(CHUNKS):
+                if rho + QLAG == r:
+                    for first, n in calls:
+                        quantise_p(c, first, n)
+            for c, (gp, k0, nk, rho, s_part, v_part, calls) in enumerate(CHUNKS):
+                if rho == r:
+                    subtract(c)
+                    loads_through(c + NW)
+            for c, (gp, k0, nk, rho, s_part, v_part, calls) in enumerate(CHUNKS):
+                if rho + 1 == r and v_part[1] > 0:
+                    regroup(c, v_part[0], v_part[1], nc.vector.tensor_copy)
+            for first, n in A_CALLS:
+                if a_round[first] == r:
+                    quantise_a(first, n)
+            for s in range(NR):
+                if ready[s] == r:
+                    second_matmul(s)
+
         nc.vector.tensor_copy(out=res[:], in_=acc[:])
         nc.sync.dma_start(out=out, in_=res[:])

@@ -25,13 +25,13 @@ FLOPS = 2 * B * KK * M * 2048 + 2 * B * KK * M * O
 PIN = False
 CHUNKS = (
     (0, 0, 2, -3, (0, 1), (1, 1), ((0, 2),)),
-    (0, 2, 3, -1, (2, 2), (4, 1), ((2, 2), (4, 1))),
-    (0, 5, 4, 3, (5, 3), (8, 1), ((5, 4),)),
-    (1, 0, 5, 8, (0, 3), (3, 2), ((0, 4), (4, 1))),
-    (1, 5, 4, 13, (5, 3), (8, 1), ((5, 4),)),
-    (2, 0, 5, 17, (0, 3), (3, 2), ((0, 4), (4, 1))),
-    (2, 5, 4, 22, (5, 3), (8, 1), ((5, 4),)),
-    (3, 0, 5, 26, (0, 3), (3, 2), ((0, 4), (4, 1))),
+    (0, 2, 3, -1, (2, 2), (4, 1), ((2, 2), (4, 1),)),
+    (0, 5, 4, 3, (5, 2), (7, 2), ((5, 4),)),
+    (1, 0, 5, 8, (0, 3), (3, 2), ((0, 4), (4, 1),)),
+    (1, 5, 4, 13, (5, 2), (7, 2), ((5, 4),)),
+    (2, 0, 5, 17, (0, 3), (3, 2), ((0, 4), (4, 1),)),
+    (2, 5, 4, 22, (5, 2), (7, 2), ((5, 4),)),
+    (3, 0, 5, 26, (0, 3), (3, 2), ((0, 4), (4, 1),)),
     (3, 5, 2, 31, (5, 1), (6, 1), ((5, 2),)),
     (3, 7, 2, 33, (7, 1), (8, 1), ((7, 2),)),
 )
@@ -59,27 +59,24 @@ def tile_convexrelucnn_w_kernel(tc, x, G_words, G_scales, v, w, out):
         psum_out = ctx.enter_context(tc.psum_pool(name="psum_out", bufs=1))
 
         w_planes = keep.tile([P, M], U8, align_bytes=64)
-        u_codes = keep.tile([P, 24 * P], U32, align_bytes=64)
-        u_planes = keep.tile([P, 24 * P], U8, align_bytes=64)
+        u_codes = keep.tile([P, KK * 512], U32, align_bytes=64)
+        u_planes = keep.tile([P, KK * 512], U8, align_bytes=64)
         p_codes = keep.tile([P, NR * O], U32, align_bytes=64)
         p_planes = keep.tile([P, NR * O], U8, align_bytes=64)
         res = keep.tile([P, O], F32)
         acc = psum_out.tile([P, O], F32)
 
-        g_rows = G_words.rearrange("g p m t -> (g p) (m t)").rearrange(
-            "(s q r) x -> q s r x", q=NG, r=8
-        )
+        g_bytes = G_words.rearrange("g p m t -> p g (m t)")
         w_codes = {}
         v_tiles = {}
         w_tiles = {}
 
         def load_w_codes(gp):
             wc = keep.tile([P, NG, 512], U32, name="wc%d" % gp, align_bytes=64)
-            for q in range(NG):
-                nc.sync.dma_start(
-                    out=wc[:, q, :].bitcast(I32),
-                    in_=g_rows[q][:, :, 2048 * gp : 2048 * (gp + 1)].bitcast(I32),
-                )
+            nc.sync.dma_start(
+                out=wc[:].bitcast(I32),
+                in_=g_bytes[:, :, 2048 * gp : 2048 * (gp + 1)].bitcast(I32),
+            )
             w_codes[gp] = wc
 
         def load_chunk(c):
@@ -113,65 +110,57 @@ def tile_convexrelucnn_w_kernel(tc, x, G_words, G_scales, v, w, out):
             x_sb = early.tile([P, H * W], BF16, align_bytes=64)
             nc.sync.dma_start(out=x_sb[:], in_=x.rearrange("b c h w -> b (c h w)"))
             nc.vector.memset(w_planes[:].bitcast(I32), 0)
-            s_rows = G_scales.rearrange("g q m -> (g q) m").rearrange(
-                "(a r q) m -> a q r m", r=4, q=NG
-            )
             for a in range(4):
                 nc.sync.dma_start(
                     out=w_planes[32 * a : 32 * a + 16, :].bitcast(I32),
-                    in_=s_rows[a].bitcast(I32),
+                    in_=G_scales[:, 4 * a : 4 * a + 4, :].bitcast(I32),
                 )
             ident = early.tile([P, P], F32)
             make_identity(nc, ident[:])
             loads_through(PRELOAD)
 
-            xs = early.tile([P, 5, 2, 2, 17 * 8], F32)
+            xs = early.tile([P, 5, H * 16], F32)
             xw = x_sb[:].bitcast(F32).rearrange("b (r c) -> b r c", c=W // 2)
             xb = x_sb[:].rearrange("b (r c) -> b r c", c=W)
-            even0 = xw[:, :, 0:32].rearrange("b (r a) (h c u) -> b u a h r c", a=2, h=2, u=2)
-            even2 = xw[:, :, 1:33].rearrange("b (r a) (h c u) -> b u a h r c", a=2, h=2, u=2)
-            odd = xb[:, :, 1:65].rearrange("b (r a) (h c u e) -> b u a h r c e", a=2, h=2, u=2, e=2)
-            for u in range(2):
-                nc.vector.tensor_copy(
-                    out=xs[:, u].rearrange("b a h (r c) -> b a h r c", c=8), in_=even0[:, u]
-                )
-            for par in range(2):
-                nc.scalar.copy(
-                    out=xs[:, 2, par].rearrange("b h (r c) -> b h r c", c=8), in_=even2[:, 1, par]
-                )
-            for par in range(2):
-                nc.vector.tensor_copy(
-                    out=xs[:, 3, par].bitcast(BF16).rearrange("b h (r c e) -> b h r c e", c=8, e=2),
-                    in_=odd[:, 0, par],
-                )
-                for h in range(2):
-                    nc.scalar.copy(
-                        out=xs[:, 4, par, h].bitcast(BF16).rearrange("b (r c e) -> b r c e", c=8, e=2),
-                        in_=odd[:, 1, par, h],
-                    )
+            even0 = xw[:, :, 0:32].rearrange("b r (c u) -> b u r c", u=2)
+            even2 = xw[:, :, 1:33].rearrange("b r (c u) -> b u r c", u=2)
+            odd = xb[:, :, 1:65].rearrange("b r (c u e) -> b u r c e", u=2, e=2)
+            nc.vector.tensor_copy(out=xs[:, 0].rearrange("b (r c) -> b r c", c=16), in_=even0[:, 0])
+            nc.scalar.copy(out=xs[:, 2].rearrange("b (r c) -> b r c", c=16), in_=even2[:, 1])
+            nc.vector.tensor_copy(out=xs[:, 1].rearrange("b (r c) -> b r c", c=16), in_=even0[:, 1])
+            nc.vector.tensor_copy(
+                out=xs[:, 3].bitcast(BF16).rearrange("b (r c e) -> b r c e", c=16, e=2), in_=odd[:, 0]
+            )
+            nc.scalar.copy(
+                out=xs[:, 4].bitcast(BF16).rearrange("b (r c e) -> b r c e", c=16, e=2), in_=odd[:, 1]
+            )
 
             n_bank = 0
-            for j in (0, 2, 1):
+            for first in range(0, KK, 2):
+                n_k = min(2, KK - first)
                 su = stream.tile([P, 4096], BF16, name="su", tag="stg", bufs=NSTG, align_bytes=64)
                 su_words = su[:].bitcast(F32).rearrange("p (g b u) -> p g b u", g=8, u=2)
-                for rho in range(4):
-                    pt = psum.tile([P, 2, 2, P], F32, name="pt", tag="bank")
+                for n in range(first, first + n_k):
+                    i, j = divmod(K_ORDER[n], 3)
                     for h in range(2):
-                        c0 = 8 * (rho // 2)
-                        for u in range(2):
-                            nc.tensor.transpose(
-                                pt[:, h, u, :], xs[:, PLANE[j][u], rho % 2, h, c0 : c0 + P], ident[:]
-                            )
-                    src = pt[:].rearrange("p s u b -> p s b u")
-                    if n_bank % 4 == 0:
-                        nc.vector.tensor_copy(out=su_words[:, 2 * rho : 2 * rho + 2], in_=src)
-                    else:
-                        nc.scalar.copy(out=su_words[:, 2 * rho : 2 * rho + 2], in_=src)
-                    n_bank += 1
+                        pt = psum.tile([P, 2, 2, P], F32, name="pt", tag="bank")
+                        for gl in range(2):
+                            c0 = (8 * (2 * h + gl) + i) * 16
+                            for u in range(2):
+                                nc.tensor.transpose(
+                                    pt[:, gl, u, :], xs[:, PLANE[j][u], c0 : c0 + P], ident[:]
+                                )
+                        src = pt[:].rearrange("p s u b -> p s b u")
+                        t0 = 4 * (n - first) + 2 * h
+                        if n_bank % 6 == 0:
+                            nc.vector.tensor_copy(out=su_words[:, t0 : t0 + 2], in_=src)
+                        else:
+                            nc.scalar.copy(out=su_words[:, t0 : t0 + 2], in_=src)
+                        n_bank += 1
                 nc.vector.quantize_mx(
-                    out=u_codes[:, j * 1024 : (j + 1) * 1024].bitcast(FP8X4),
-                    scales=u_planes[:, j * 1024 : (j + 1) * 1024],
-                    in_=su[:],
+                    out=u_codes[:, first * 512 : (first + n_k) * 512].bitcast(FP8X4),
+                    scales=u_planes[:, first * 512 : (first + n_k) * 512],
+                    in_=su[:, 0 : n_k * 2048],
                 )
 
         late = ctx.enter_context(tc.tile_pool(name="late", bufs=1))
@@ -187,12 +176,11 @@ def tile_convexrelucnn_w_kernel(tc, x, G_words, G_scales, v, w, out):
 
         def first_matmul(s):
             gp, n = divmod(s, KK)
-            i, j = divmod(K_ORDER[n], 3)
             bank = psum.tile([P, 4, P], F32, name="bank", tag="bank")
             for t in range(4):
                 m0 = 512 * gp + 128 * t
                 for g in range(NG):
-                    u0 = (8 * j + 2 * (g // 2 + i) + g % 2) * P
+                    u0 = (4 * n + g) * P
                     nc.tensor.matmul_mx(
                         out=bank[:, t, :],
                         lhsT=w_codes[gp][:, g, 128 * t : 128 * (t + 1)].bitcast(FP8X4),
@@ -208,7 +196,7 @@ def tile_convexrelucnn_w_kernel(tc, x, G_words, G_scales, v, w, out):
             first, n = call_of[s]
             if s == first:
                 a_stage[first] = stream.tile(
-                    [P, 4, P, 4], BF16, name="ag", tag="ag", bufs=3, align_bytes=64
+                    [P, 4, P, 4], BF16, name="ag", tag="ag", bufs=2, align_bytes=64
                 )
             nc.scalar.copy(
                 out=a_stage[first][:, s - first], in_=banks[s][:].rearrange("p t b -> p b t")

@@ -11,293 +11,204 @@ U8 = mybir.dt.uint8
 FP8X4 = mybir.dt.float8_e4m3fn_x4
 
 P = 128
-B = 128
-H = 34
-W = 66
-KK = 9
-M = 2048
-O = 256
-NG = 4
-MG = 4
-NR = MG * KK
-FLOPS = 2 * B * KK * M * 2048 + 2 * B * KK * M * O
+ROWS = 34
+COLS = 66
+TAPS = 9
+NEURONS = 2048
+OUTS = 256
+PASSES = 4
+GROUPS = 4
+PACK = 4
+ROW_WORDS = 16
+FLOPS = 2 * P * TAPS * NEURONS * 2048 + 2 * P * TAPS * NEURONS * OUTS
 
-PIN = False
-CHUNKS = (
-    (0, 0, 2, -3, (0, 1), (1, 1), ((0, 2),)),
-    (0, 2, 3, -1, (2, 2), (4, 1), ((2, 2), (4, 1),)),
-    (0, 5, 4, 3, (5, 2), (7, 2), ((5, 4),)),
-    (1, 0, 5, 8, (0, 3), (3, 2), ((0, 4), (4, 1),)),
-    (1, 5, 4, 13, (5, 2), (7, 2), ((5, 4),)),
-    (2, 0, 5, 17, (0, 3), (3, 2), ((0, 4), (4, 1),)),
-    (2, 5, 4, 22, (5, 2), (7, 2), ((5, 4),)),
-    (3, 0, 5, 26, (0, 3), (3, 2), ((0, 4), (4, 1),)),
-    (3, 5, 2, 31, (5, 1), (6, 1), ((5, 2),)),
-    (3, 7, 2, 33, (7, 1), (8, 1), ((7, 2),)),
-)
-A_CALLS = ((0, 4), (4, 4), (8, 4), (12, 4), (16, 4), (20, 4), (24, 4), (28, 4), (32, 2), (34, 1), (35, 1))
-K_ORDER = (0, 3, 6, 2, 5, 8, 1, 4, 7)
-PLANE = ((0, 1), (3, 4), (1, 2))
-LOAD_SEQ = (("c", 0), ("w", 0), ("c", 1), ("c", 2), ("w", 1), ("c", 3), ("c", 4), ("w", 2), ("c", 5), ("c", 6), ("w", 3), ("c", 7), ("c", 8), ("c", 9))
-PRELOAD = 2
-MAXK = 5
-NV = 4
-NW = 3
-NSTG = 3
-QLAG = 4
-PASS_LAG = 1
+A_RUNS = ((0, 4), (4, 4), (8, 1))
+P_RUNS = ((0, 4, 2), (4, 4, 2), (8, 1, 1))
 
 
 def tile_convexrelucnn_w_kernel(tc, x, G_words, G_scales, v, w, out):
     nc = tc.nc
     with ExitStack() as ctx:
-        if PIN:
-            ctx.enter_context(tc.manual_schedule())
         keep = ctx.enter_context(tc.tile_pool(name="keep", bufs=1))
         stream = ctx.enter_context(tc.tile_pool(name="stream", bufs=2))
         psum = ctx.enter_context(tc.psum_pool(name="psum", bufs=7))
         psum_out = ctx.enter_context(tc.psum_pool(name="psum_out", bufs=1))
 
-        w_planes = keep.tile([P, M], U8, align_bytes=64)
-        u_codes = keep.tile([P, KK * 512], U32, align_bytes=64)
-        u_planes = keep.tile([P, KK * 512], U8, align_bytes=64)
-        p_codes = keep.tile([P, NR * O], U32, align_bytes=64)
-        p_planes = keep.tile([P, NR * O], U8, align_bytes=64)
-        res = keep.tile([P, O], F32)
-        acc = psum_out.tile([P, O], F32)
+        g_planes = keep.tile([P, NEURONS], U8, align_bytes=64)
+        u_codes = keep.tile([P, TAPS, PASSES, P], U32, align_bytes=64)
+        u_planes = keep.tile([P, TAPS, PASSES, P], U8, align_bytes=64)
+        p_codes = keep.tile([P, GROUPS * TAPS, OUTS], U32, align_bytes=64)
+        p_planes = keep.tile([P, GROUPS * TAPS, OUTS], U8, align_bytes=64)
+        result = keep.tile([P, OUTS], F32)
+        out_sum = psum_out.tile([P, OUTS], F32)
 
-        g_bytes = G_words.rearrange("g p m t -> p g (m t)")
-        w_codes = {}
-        v_tiles = {}
-        w_tiles = {}
+        g_codes = []
+        v_groups = {}
+        w_groups = {}
 
-        def load_w_codes(gp):
-            wc = keep.tile([P, NG, 512], U32, name="wc%d" % gp, align_bytes=64)
+        def load_g_half(half):
+            codes = keep.tile([P, PASSES, NEURONS // 2], U32, name="g_codes%d" % half, align_bytes=64)
+            lo = half * 2 * NEURONS
             nc.sync.dma_start(
-                out=wc[:].bitcast(I32),
-                in_=g_bytes[:, :, 2048 * gp : 2048 * (gp + 1)].bitcast(I32),
+                out=codes[:].bitcast(I32),
+                in_=G_words.rearrange("g r m t -> r g (m t)")[:, :, lo : lo + 2 * NEURONS].bitcast(I32),
             )
-            w_codes[gp] = wc
+            g_codes.append(codes)
 
-        def load_chunk(c):
-            gp, k0, nk = CHUNKS[c][0:3]
-            vc = stream.tile([P, 4, MAXK * O], BF16, name="vc", tag="vc", bufs=NV)
-            wn = stream.tile([P, 4, MAXK * O], BF16, name="wn", tag="wn", bufs=NW)
-            for dst, src in ((vc, v), (wn, w)):
-                nc.sync.dma_start(
-                    out=dst[:, :, 0 : nk * O],
-                    in_=src[512 * gp : 512 * (gp + 1), k0 : k0 + nk, :].rearrange(
-                        "(t p) k o -> p t (k o)", p=P
-                    ),
-                )
-            v_tiles[c] = vc
-            w_tiles[c] = wn
-
-        load_pos = [0]
-
-        def loads_through(c):
-            while load_pos[0] < len(LOAD_SEQ):
-                kind, n = LOAD_SEQ[load_pos[0]]
-                if kind == "c" and n > c:
-                    break
-                load_pos[0] += 1
-                if kind == "c":
-                    load_chunk(n)
-                else:
-                    load_w_codes(n)
+        def load_group(e):
+            v_group = stream.tile([P, PACK, TAPS * OUTS], BF16, name="v_group")
+            w_group = stream.tile([P, PACK, TAPS * OUTS], BF16, name="w_group")
+            for t in range(PACK):
+                m0 = 512 * e + P * t
+                nc.sync.dma_start(out=v_group[:, t, :], in_=v[m0 : m0 + P].rearrange("r k o -> r (k o)"))
+                nc.sync.dma_start(out=w_group[:, t, :], in_=w[m0 : m0 + P].rearrange("r k o -> r (k o)"))
+            v_groups[e] = v_group
+            w_groups[e] = w_group
 
         with tc.tile_pool(name="early", bufs=1) as early:
-            x_sb = early.tile([P, H * W], BF16, align_bytes=64)
+            x_sb = early.tile([P, ROWS * COLS], BF16, align_bytes=64)
             nc.sync.dma_start(out=x_sb[:], in_=x.rearrange("b c h w -> b (c h w)"))
-            nc.vector.memset(w_planes[:].bitcast(I32), 0)
+
+            nc.vector.memset(g_planes[:].bitcast(I32), 0)
             for a in range(4):
                 nc.sync.dma_start(
-                    out=w_planes[32 * a : 32 * a + 16, :].bitcast(I32),
+                    out=g_planes[32 * a : 32 * a + 16, :].bitcast(I32),
                     in_=G_scales[:, 4 * a : 4 * a + 4, :].bitcast(I32),
                 )
-            ident = early.tile([P, P], F32)
-            make_identity(nc, ident[:])
-            loads_through(PRELOAD)
+            load_g_half(0)
+            load_group(0)
+            load_group(1)
+            load_g_half(1)
 
-            xs = early.tile([P, 5, H * 16], F32)
-            xw = x_sb[:].bitcast(F32).rearrange("b (r c) -> b r c", c=W // 2)
-            xb = x_sb[:].rearrange("b (r c) -> b r c", c=W)
-            even0 = xw[:, :, 0:32].rearrange("b r (c u) -> b u r c", u=2)
-            even2 = xw[:, :, 1:33].rearrange("b r (c u) -> b u r c", u=2)
-            odd = xb[:, :, 1:65].rearrange("b r (c u e) -> b u r c e", u=2, e=2)
-            nc.vector.tensor_copy(out=xs[:, 0].rearrange("b (r c) -> b r c", c=16), in_=even0[:, 0])
-            nc.scalar.copy(out=xs[:, 2].rearrange("b (r c) -> b r c", c=16), in_=even2[:, 1])
-            nc.vector.tensor_copy(out=xs[:, 1].rearrange("b (r c) -> b r c", c=16), in_=even0[:, 1])
-            nc.vector.tensor_copy(
-                out=xs[:, 3].bitcast(BF16).rearrange("b (r c e) -> b r c e", c=16, e=2), in_=odd[:, 0]
-            )
-            nc.scalar.copy(
-                out=xs[:, 4].bitcast(BF16).rearrange("b (r c e) -> b r c e", c=16, e=2), in_=odd[:, 1]
+            identity = early.tile([P, P], F32)
+            make_identity(nc, identity[:])
+
+            pairs = early.tile([P, 5, ROWS * ROW_WORDS], F32)
+            x_words = x_sb[:].bitcast(F32).rearrange("b (h c) -> b h c", c=COLS // 2)
+            odd = x_sb[:].rearrange("b (h c) -> b h c", c=COLS)[:, :, 1:65].rearrange(
+                "b h (c u e) -> b u h c e", u=2, e=2
             )
 
-            n_bank = 0
-            for first in range(0, KK, 2):
-                n_k = min(2, KK - first)
-                su = stream.tile([P, 4096], BF16, name="su", tag="stg", bufs=NSTG, align_bytes=64)
-                su_words = su[:].bitcast(F32).rearrange("p (g b u) -> p g b u", g=8, u=2)
-                for n in range(first, first + n_k):
-                    i, j = divmod(K_ORDER[n], 3)
-                    for h in range(2):
-                        pt = psum.tile([P, 2, 2, P], F32, name="pt", tag="bank")
-                        for gl in range(2):
-                            c0 = (8 * (2 * h + gl) + i) * 16
+            def sort_even(copy, s, first_word, u):
+                copy(
+                    out=pairs[:, s].rearrange("b (h c) -> b h c", c=ROW_WORDS),
+                    in_=x_words[:, :, first_word : first_word + 32].rearrange("b h (c u) -> b u h c", u=2)[:, u],
+                )
+
+            def sort_odd(copy, s, u):
+                copy(
+                    out=pairs[:, s].bitcast(BF16).rearrange("b (h c e) -> b h c e", c=ROW_WORDS, e=2),
+                    in_=odd[:, u],
+                )
+
+            sort_even(nc.vector.tensor_copy, 0, 0, 0)
+            sort_odd(nc.scalar.copy, 3, 1)
+            sort_even(nc.vector.tensor_copy, 2, 0, 1)
+            sort_odd(nc.vector.tensor_copy, 1, 0)
+            sort_even(nc.scalar.copy, 4, 1, 1)
+
+            for k0 in range(0, TAPS, 2):
+                n_k = min(2, TAPS - k0)
+                grouped = stream.tile([P, 4096], BF16, name="grouped", bufs=3, align_bytes=64)
+                words = grouped[:].bitcast(F32).rearrange("r (k g b u) -> r k g b u", k=2, g=PASSES, u=2)
+                for k in range(k0, k0 + n_k):
+                    i, j = divmod(k, 3)
+                    for g0 in range(0, PASSES, 2):
+                        flipped = psum.tile([P, 2, 2, P], F32, name="flipped", tag="bank")
+                        for g in range(g0, g0 + 2):
+                            first = (8 * g + i) * ROW_WORDS
                             for u in range(2):
                                 nc.tensor.transpose(
-                                    pt[:, gl, u, :], xs[:, PLANE[j][u], c0 : c0 + P], ident[:]
+                                    flipped[:, g - g0, u, :], pairs[:, j + 2 * u, first : first + P], identity[:]
                                 )
-                        src = pt[:].rearrange("p s u b -> p s b u")
-                        t0 = 4 * (n - first) + 2 * h
-                        if n_bank % 6 == 0:
-                            nc.vector.tensor_copy(out=su_words[:, t0 : t0 + 2], in_=src)
-                        else:
-                            nc.scalar.copy(out=su_words[:, t0 : t0 + 2], in_=src)
-                        n_bank += 1
+                        nc.scalar.copy(
+                            out=words[:, k - k0, g0 : g0 + 2], in_=flipped[:].rearrange("r g u b -> r g b u")
+                        )
                 nc.vector.quantize_mx(
-                    out=u_codes[:, first * 512 : (first + n_k) * 512].bitcast(FP8X4),
-                    scales=u_planes[:, first * 512 : (first + n_k) * 512],
-                    in_=su[:, 0 : n_k * 2048],
+                    out=u_codes[:, k0 : k0 + n_k].rearrange("r k g b -> r (k g b)").bitcast(FP8X4),
+                    scales=u_planes[:, k0 : k0 + n_k].rearrange("r k g b -> r (k g b)"),
+                    in_=grouped[:, 0 : n_k * 2048],
                 )
 
         late = ctx.enter_context(tc.tile_pool(name="late", bufs=1))
-        a_codes = late.tile([P, NR * P], U32, align_bytes=64)
-        a_planes = late.tile([P, NR * P], U8, align_bytes=64)
+        a_codes = late.tile([P, GROUPS * TAPS, P], U32, align_bytes=64)
+        a_planes = late.tile([P, GROUPS * TAPS, P], U8, align_bytes=64)
 
-        banks = {}
-        a_stage = {}
-        call_of = {}
-        for first, n in A_CALLS:
-            for s in range(first, first + n):
-                call_of[s] = (first, n)
-
-        def first_matmul(s):
-            gp, n = divmod(s, KK)
-            bank = psum.tile([P, 4, P], F32, name="bank", tag="bank")
-            for t in range(4):
-                m0 = 512 * gp + 128 * t
-                for g in range(NG):
-                    u0 = (4 * n + g) * P
-                    nc.tensor.matmul_mx(
-                        out=bank[:, t, :],
-                        lhsT=w_codes[gp][:, g, 128 * t : 128 * (t + 1)].bitcast(FP8X4),
-                        lhsT_scale=w_planes[4 * g : P, m0 : m0 + 128],
-                        rhs=u_codes[:, u0 : u0 + P].bitcast(FP8X4),
-                        rhs_scale=u_planes[:, u0 : u0 + P],
-                        start=(g == 0),
-                        stop=(g == NG - 1),
-                    )
-            banks[s] = bank
-
-        def leave_psum(s):
-            first, n = call_of[s]
-            if s == first:
-                a_stage[first] = stream.tile(
-                    [P, 4, P, 4], BF16, name="ag", tag="ag", bufs=2, align_bytes=64
+        def first_product(e):
+            for k0, n_k in A_RUNS:
+                a_grouped = stream.tile([P, 4, P, PACK], BF16, name="a_grouped", align_bytes=64)
+                for k in range(k0, k0 + n_k):
+                    bank = psum.tile([P, PACK, P], F32, name="bank", tag="bank")
+                    for t in range(PACK):
+                        m0 = 512 * e + P * t
+                        c0 = m0 % (NEURONS // 2)
+                        for g in range(PASSES):
+                            nc.tensor.matmul_mx(
+                                out=bank[:, t, :],
+                                lhsT=g_codes[e // 2][:, g, c0 : c0 + P].bitcast(FP8X4),
+                                lhsT_scale=g_planes[4 * g : P, m0 : m0 + P],
+                                rhs=u_codes[:, k, g, :].bitcast(FP8X4),
+                                rhs_scale=u_planes[:, k, g, :],
+                                start=(g == 0),
+                                stop=(g == PASSES - 1),
+                            )
+                    nc.scalar.copy(out=a_grouped[:, k - k0], in_=bank[:].rearrange("r t b -> r b t"))
+                s0 = e * TAPS + k0
+                nc.vector.quantize_mx(
+                    out=a_codes[:, s0 : s0 + n_k].rearrange("r s b -> r (s b)").bitcast(FP8X4),
+                    scales=a_planes[:, s0 : s0 + n_k].rearrange("r s b -> r (s b)"),
+                    in_=a_grouped[:, 0:n_k].rearrange("r s b t -> r (s b t)"),
                 )
-            nc.scalar.copy(
-                out=a_stage[first][:, s - first], in_=banks[s][:].rearrange("p t b -> p b t")
-            )
 
-        def quantise_a(first, n):
-            nc.vector.quantize_mx(
-                out=a_codes[:, first * P : (first + n) * P].bitcast(FP8X4),
-                scales=a_planes[:, first * P : (first + n) * P],
-                in_=a_stage[first][:, 0:n].rearrange("p s b t -> p (s b t)"),
-            )
-
-        p_stage = {}
-
-        def subtract(c):
-            nk = CHUNKS[c][2]
-            nc.vector.tensor_tensor(
-                out=v_tiles[c][:, :, 0 : nk * O],
-                in0=v_tiles[c][:, :, 0 : nk * O],
-                in1=w_tiles[c][:, :, 0 : nk * O],
-                op=mybir.AluOpType.subtract,
-            )
-            p_stage[c] = stream.tile(
-                [P, MAXK * 1024], BF16, name="pg", tag="stg", bufs=NSTG, align_bytes=64
-            )
-
-        def regroup(c, first, n, copy):
-            lo = first - CHUNKS[c][1]
+        def regroup(copy, grouped, v_group, k0, first, n_k):
             copy(
-                out=p_stage[c][:, lo * 1024 : (lo + n) * 1024].rearrange(
-                    "p (c i t) -> p c t i", i=4, t=4
+                out=grouped[:, (first - k0) * 1024 : (first - k0 + n_k) * 1024].rearrange(
+                    "r (c i t) -> r c t i", i=4, t=PACK
                 ),
-                in_=v_tiles[c][:, :, lo * O : (lo + n) * O].rearrange("p t (c i) -> p c t i", i=4),
+                in_=v_group[:, :, first * OUTS : (first + n_k) * OUTS].rearrange("r t (c i) -> r c t i", i=4),
             )
 
-        def quantise_p(c, first, n):
-            gp, k0 = CHUNKS[c][0:2]
-            c0 = (gp * KK + first) * O
-            nc.vector.quantize_mx(
-                out=p_codes[:, c0 : c0 + n * O].bitcast(FP8X4),
-                scales=p_planes[:, c0 : c0 + n * O],
-                in_=p_stage[c][:, (first - k0) * 1024 : (first - k0 + n) * 1024],
-            )
+        def difference(e):
+            v_group = v_groups[e]
+            for t in range(PACK):
+                nc.vector.tensor_tensor(
+                    out=v_group[:, t, :],
+                    in0=v_group[:, t, :],
+                    in1=w_groups[e][:, t, :],
+                    op=mybir.AluOpType.subtract,
+                )
+            for k0, n_k, n_scalar in P_RUNS:
+                grouped = stream.tile([P, 4096], BF16, name="grouped", bufs=3, align_bytes=64)
+                regroup(nc.scalar.copy, grouped, v_group, k0, k0, n_scalar)
+                if n_k > n_scalar:
+                    regroup(nc.vector.tensor_copy, grouped, v_group, k0, k0 + n_scalar, n_k - n_scalar)
+                s0 = e * TAPS + k0
+                nc.vector.quantize_mx(
+                    out=p_codes[:, s0 : s0 + n_k].rearrange("r s o -> r (s o)").bitcast(FP8X4),
+                    scales=p_planes[:, s0 : s0 + n_k].rearrange("r s o -> r (s o)"),
+                    in_=grouped[:, 0 : n_k * 1024],
+                )
 
-        passes_done = [0]
+        def second_product(e):
+            for s in range(e * TAPS, (e + 1) * TAPS):
+                nc.tensor.matmul_mx(
+                    out=out_sum[:],
+                    lhsT=a_codes[:, s, :].bitcast(FP8X4),
+                    lhsT_scale=a_planes[:, s, :],
+                    rhs=p_codes[:, s, :].bitcast(FP8X4),
+                    rhs_scale=p_planes[:, s, :],
+                    start=(s == 0),
+                    stop=(s == GROUPS * TAPS - 1),
+                )
 
-        def second_matmul(s):
-            ra = (s // KK) * KK + K_ORDER.index(s % KK)
-            nc.tensor.matmul_mx(
-                out=acc[:],
-                lhsT=a_codes[:, ra * P : (ra + 1) * P].bitcast(FP8X4),
-                lhsT_scale=a_planes[:, ra * P : (ra + 1) * P],
-                rhs=p_codes[:, s * O : (s + 1) * O].bitcast(FP8X4),
-                rhs_scale=p_planes[:, s * O : (s + 1) * O],
-                start=(passes_done[0] == 0),
-                stop=(passes_done[0] == NR - 1),
-            )
-            passes_done[0] += 1
+        for e in range(GROUPS):
+            first_product(e)
+            difference(e)
+            if e + 2 < GROUPS:
+                load_group(e + 2)
+            if e > 0:
+                second_product(e - 1)
+        second_product(GROUPS - 1)
 
-        a_round = {}
-        for first, n in A_CALLS:
-            lag = 2 if first + n < NR - 3 else 1
-            for s in range(first, first + n):
-                a_round[s] = first + n - 1 + lag
-        p_round = {}
-        for gp, k0, nk, rho, s_part, v_part, calls in CHUNKS:
-            for k in range(k0, k0 + nk):
-                p_round[gp * KK + k] = rho + QLAG
-        ready = {}
-        for s in range(NR):
-            ready[s] = max(a_round[(s // KK) * KK + K_ORDER.index(s % KK)], p_round[s])
-            if ready[s] < NR - 3:
-                ready[s] += PASS_LAG
-        first_round = min(c[3] for c in CHUNKS)
-        last_round = max(ready[s] for s in range(NR))
-
-        for r in range(min(first_round, 0), last_round + 1):
-            if 0 <= r < NR:
-                first_matmul(r)
-            for c, (gp, k0, nk, rho, s_part, v_part, calls) in enumerate(CHUNKS):
-                if rho + 1 == r and s_part[1] > 0:
-                    regroup(c, s_part[0], s_part[1], nc.scalar.copy)
-            if 0 <= r < NR:
-                leave_psum(r)
-            for c, (gp, k0, nk, rho, s_part, v_part, calls) in enumerate(CHUNKS):
-                if rho + QLAG == r:
-                    for first, n in calls:
-                        quantise_p(c, first, n)
-            for c, (gp, k0, nk, rho, s_part, v_part, calls) in enumerate(CHUNKS):
-                if rho == r:
-                    subtract(c)
-                    loads_through(c + NW)
-            for c, (gp, k0, nk, rho, s_part, v_part, calls) in enumerate(CHUNKS):
-                if rho + 1 == r and v_part[1] > 0:
-                    regroup(c, v_part[0], v_part[1], nc.vector.tensor_copy)
-            for first, n in A_CALLS:
-                if a_round[first] == r:
-                    quantise_a(first, n)
-            for s in range(NR):
-                if ready[s] == r:
-                    second_matmul(s)
-
-        nc.vector.tensor_copy(out=res[:], in_=acc[:])
-        nc.sync.dma_start(out=out, in_=res[:])
+        nc.vector.tensor_copy(out=result[:], in_=out_sum[:])
+        nc.sync.dma_start(out=out, in_=result[:])

@@ -23,7 +23,14 @@ ROW_WORDS = 16
 FLOPS = 2 * P * TAPS * NEURONS * 2048 + 2 * P * TAPS * NEURONS * OUTS
 
 A_RUNS = ((0, 4), (4, 4), (8, 1))
-P_RUNS = ((0, 4, 2), (4, 4, 2), (8, 1, 1))
+P_RUNS = ((0, 2), (2, 2), (4, 2), (6, 2), (8, 1))
+VECTOR_TAPS = (1, 3, 5, 7)
+STEPS = GROUPS * TAPS
+AHEAD = 2
+
+
+def p_step(e, k):
+    return 1 + (e * TAPS + k) * 1 // 1
 
 
 def tile_convexrelucnn_w_kernel(tc, x, G_words, G_scales, v, w, out):
@@ -37,178 +44,243 @@ def tile_convexrelucnn_w_kernel(tc, x, G_words, G_scales, v, w, out):
         g_planes = keep.tile([P, NEURONS], U8, align_bytes=64)
         u_codes = keep.tile([P, TAPS, PASSES, P], U32, align_bytes=64)
         u_planes = keep.tile([P, TAPS, PASSES, P], U8, align_bytes=64)
-        p_codes = keep.tile([P, GROUPS * TAPS, OUTS], U32, align_bytes=64)
-        p_planes = keep.tile([P, GROUPS * TAPS, OUTS], U8, align_bytes=64)
         result = keep.tile([P, OUTS], F32)
+        identity = keep.tile([P, P], F32)
+        x_sb = stream.tile([P, ROWS * COLS], BF16, name="x_sb", tag="a_codes", align_bytes=64)
+        pairs = stream.tile([P, 5, ROWS * ROW_WORDS], F32, name="pairs", tag="p_codes", align_bytes=64)
         out_sum = psum_out.tile([P, OUTS], F32)
 
         g_codes = []
-        v_groups = {}
-        w_groups = {}
+        parts = {}
+        a_groups = {}
+        p_groups = {}
+        a_runs = {}
+        p_runs = {}
 
-        def load_g_half(half):
-            codes = keep.tile([P, PASSES, NEURONS // 2], U32, name="g_codes%d" % half, align_bytes=64)
-            lo = half * 2 * NEURONS
+        def load_g(e):
+            codes = keep.tile([P, PASSES, 512], U32, name="g_codes%d" % e, align_bytes=64)
             nc.sync.dma_start(
                 out=codes[:].bitcast(I32),
-                in_=G_words.rearrange("g r m t -> r g (m t)")[:, :, lo : lo + 2 * NEURONS].bitcast(I32),
+                in_=G_words.rearrange("g r m t -> r g (m t)")[:, :, e * 2048 : (e + 1) * 2048].bitcast(I32),
             )
             g_codes.append(codes)
 
-        def load_group(e):
-            v_group = stream.tile([P, PACK, TAPS * OUTS], BF16, name="v_group")
-            w_group = stream.tile([P, PACK, TAPS * OUTS], BF16, name="w_group")
+        def load_taps(e, k0, n_k):
+            v_part = keep.tile([P, PACK, n_k * OUTS], BF16, name="v_taps%d_%d" % (e % 3, k0), align_bytes=64)
+            w_part = keep.tile([P, PACK, n_k * OUTS], BF16, name="w_taps%d_%d" % (e % 3, k0), align_bytes=64)
             for t in range(PACK):
                 m0 = 512 * e + P * t
-                nc.sync.dma_start(out=v_group[:, t, :], in_=v[m0 : m0 + P].rearrange("r k o -> r (k o)"))
-                nc.sync.dma_start(out=w_group[:, t, :], in_=w[m0 : m0 + P].rearrange("r k o -> r (k o)"))
-            v_groups[e] = v_group
-            w_groups[e] = w_group
+                nc.sync.dma_start(
+                    out=v_part[:, t, :], in_=v[m0 : m0 + P, k0 : k0 + n_k].rearrange("r k o -> r (k o)")
+                )
+                nc.sync.dma_start(
+                    out=w_part[:, t, :], in_=w[m0 : m0 + P, k0 : k0 + n_k].rearrange("r k o -> r (k o)")
+                )
+            for k in range(k0, k0 + n_k):
+                parts[e, k] = (v_part, w_part, k - k0)
 
-        with tc.tile_pool(name="early", bufs=1) as early:
-            x_sb = early.tile([P, ROWS * COLS], BF16, align_bytes=64)
+        def load_group(e):
+            for k0, n_k in ((0, 4), (4, 5)) if e in (0, 3) else ((0, TAPS),):
+                load_taps(e, k0, n_k)
+
+        def sort_even(copy, s, first_word, u):
+            copy(
+                out=pairs[:, s].rearrange("b (h c) -> b h c", c=ROW_WORDS),
+                in_=x_words[:, :, first_word : first_word + 32].rearrange("b h (c u) -> b u h c", u=2)[:, u],
+            )
+
+        def sort_odd(copy, s, u):
+            copy(
+                out=pairs[:, s].bitcast(BF16).rearrange("b (h c e) -> b h c e", c=ROW_WORDS, e=2),
+                in_=odd[:, u],
+            )
+
+        u_banks = {}
+
+        def transpose_tap(k):
+            i, j = divmod(k, 3)
+            banks = []
+            for g0 in range(0, PASSES, 2):
+                flipped = psum.tile([P, 2, 2, P], F32, name="flipped", tag="bank")
+                for g in range(g0, g0 + 2):
+                    first = (8 * g + i) * ROW_WORDS
+                    for u in range(2):
+                        nc.tensor.transpose(
+                            flipped[:, g - g0, u, :], pairs[:, j + 2 * u, first : first + P], identity[:]
+                        )
+                banks.append(flipped)
+            u_banks[k] = banks
+
+        u_grouped = {}
+
+        def empty_tap(k):
+            grouped = stream.tile([P, 2048], BF16, name="grouped", bufs=4, align_bytes=64)
+            words = grouped[:, 0:2048].bitcast(F32).rearrange("r (g b u) -> r g b u", g=PASSES, u=2)
+            for half, copy in enumerate((nc.scalar.copy, nc.vector.tensor_copy)):
+                copy(
+                    out=words[:, 2 * half : 2 * half + 2],
+                    in_=u_banks[k][half][:].rearrange("r g u b -> r g b u"),
+                )
+            u_grouped[k] = grouped
+
+        def quantise_tap(k):
+            nc.vector.quantize_mx(
+                out=u_codes[:, k].rearrange("r g b -> r (g b)").bitcast(FP8X4),
+                scales=u_planes[:, k].rearrange("r g b -> r (g b)"),
+                in_=u_grouped[k][:, 0:2048],
+            )
+
+        a_banks = {}
+
+        def first_product(e, k):
+            bank = psum.tile([P, PACK, P], F32, name="bank", tag="bank")
+            for t in range(PACK):
+                m0 = 512 * e + P * t
+                for g in range(PASSES):
+                    nc.tensor.matmul_mx(
+                        out=bank[:, t, :],
+                        lhsT=g_codes[e][:, g, P * t : P * t + P].bitcast(FP8X4),
+                        lhsT_scale=g_planes[4 * g : P, m0 : m0 + P],
+                        rhs=u_codes[:, k, g, :].bitcast(FP8X4),
+                        rhs_scale=u_planes[:, k, g, :],
+                        start=(g == 0),
+                        stop=(g == PASSES - 1),
+                    )
+            a_banks[e, k] = bank
+
+        def run_of(runs, k):
+            return [run for run in runs if run[0] <= k < run[0] + run[1]][0]
+
+        def empty_a(e, k):
+            k0, n_k = run_of(A_RUNS, k)
+            if k == k0:
+                a_runs[e, k0] = stream.tile([P, 4, P, PACK], BF16, name="a_grouped", bufs=3, align_bytes=64)
+            nc.scalar.copy(out=a_runs[e, k0][:, k - k0], in_=a_banks[e, k][:].rearrange("r t b -> r b t"))
+
+        def quantise_a(e, k0, n_k):
+            if k0 == 0:
+                a_groups[e] = (
+                    stream.tile([P, TAPS, P], U32, name="a_codes", align_bytes=64),
+                    stream.tile([P, TAPS, P], U8, name="a_planes", align_bytes=64),
+                )
+            a_codes, a_planes = a_groups[e]
+            nc.vector.quantize_mx(
+                out=a_codes[:, k0 : k0 + n_k].rearrange("r s b -> r (s b)").bitcast(FP8X4),
+                scales=a_planes[:, k0 : k0 + n_k].rearrange("r s b -> r (s b)"),
+                in_=a_runs[e, k0][:, 0:n_k].rearrange("r s b t -> r (s b t)"),
+            )
+
+        def subtract(e, k):
+            v_part, w_part, at = parts[e, k]
+            cols = slice(at * OUTS, (at + 1) * OUTS)
+            nc.vector.tensor_tensor(
+                out=v_part[:, :, cols], in0=v_part[:, :, cols], in1=w_part[:, :, cols], op=mybir.AluOpType.subtract
+            )
+
+        def by_plane(e, k, which):
+            part = parts[e, k][which]
+            at = parts[e, k][2] * OUTS
+            return part[:, :, at : at + OUTS].rearrange("r t (c i) -> r c t i", i=4)
+
+        def by_out(e, k):
+            k0, n_k = run_of(P_RUNS, k)
+            if (e, k0) not in p_runs:
+                p_runs[e, k0] = stream.tile([P, 2048], BF16, name="grouped", bufs=4, align_bytes=64)
+            return p_runs[e, k0][:, (k - k0) * 1024 : (k - k0 + 1) * 1024].rearrange("r (c i t) -> r c t i", i=4, t=PACK)
+
+        def regroup(e, k):
+            if k not in VECTOR_TAPS:
+                nc.scalar.copy(out=by_out(e, k), in_=by_plane(e, k, 0))
+            else:
+                nc.vector.tensor_tensor(
+                    out=by_out(e, k), in0=by_plane(e, k, 0), in1=by_plane(e, k, 1), op=mybir.AluOpType.subtract
+                )
+
+        def quantise_p(e, k0, n_k):
+            if k0 == 0:
+                p_groups[e] = (
+                    stream.tile([P, TAPS, OUTS], U32, name="p_codes", align_bytes=64),
+                    stream.tile([P, TAPS, OUTS], U8, name="p_planes", align_bytes=64),
+                )
+            p_codes, p_planes = p_groups[e]
+            nc.vector.quantize_mx(
+                out=p_codes[:, k0 : k0 + n_k].rearrange("r s o -> r (s o)").bitcast(FP8X4),
+                scales=p_planes[:, k0 : k0 + n_k].rearrange("r s o -> r (s o)"),
+                in_=p_runs[e, k0][:, 0 : n_k * 1024],
+            )
+
+        def second_product(e, k0, n_k):
+            a_codes, a_planes = a_groups[e]
+            p_codes, p_planes = p_groups[e]
+            for k in range(k0, k0 + n_k):
+                nc.tensor.matmul_mx(
+                    out=out_sum[:],
+                    lhsT=a_codes[:, k, :].bitcast(FP8X4),
+                    lhsT_scale=a_planes[:, k, :],
+                    rhs=p_codes[:, k, :].bitcast(FP8X4),
+                    rhs_scale=p_planes[:, k, :],
+                    start=(e == 0 and k == 0),
+                    stop=(e == GROUPS - 1 and k == TAPS - 1),
+                )
+
+        with tc.manual_schedule():
             nc.sync.dma_start(out=x_sb[:], in_=x.rearrange("b c h w -> b (c h w)"))
-
             nc.vector.memset(g_planes[:].bitcast(I32), 0)
             for a in range(4):
                 nc.sync.dma_start(
                     out=g_planes[32 * a : 32 * a + 16, :].bitcast(I32),
                     in_=G_scales[:, 4 * a : 4 * a + 4, :].bitcast(I32),
                 )
-            load_g_half(0)
-            load_group(0)
-            load_group(1)
-            load_g_half(1)
-
-            identity = early.tile([P, P], F32)
             make_identity(nc, identity[:])
+            for e in range(3):
+                load_g(e)
+                load_group(e)
+            load_g(3)
 
-            pairs = early.tile([P, 5, ROWS * ROW_WORDS], F32)
             x_words = x_sb[:].bitcast(F32).rearrange("b (h c) -> b h c", c=COLS // 2)
             odd = x_sb[:].rearrange("b (h c) -> b h c", c=COLS)[:, :, 1:65].rearrange(
                 "b h (c u e) -> b u h c e", u=2, e=2
             )
-
-            def sort_even(copy, s, first_word, u):
-                copy(
-                    out=pairs[:, s].rearrange("b (h c) -> b h c", c=ROW_WORDS),
-                    in_=x_words[:, :, first_word : first_word + 32].rearrange("b h (c u) -> b u h c", u=2)[:, u],
-                )
-
-            def sort_odd(copy, s, u):
-                copy(
-                    out=pairs[:, s].bitcast(BF16).rearrange("b (h c e) -> b h c e", c=ROW_WORDS, e=2),
-                    in_=odd[:, u],
-                )
-
             sort_even(nc.vector.tensor_copy, 0, 0, 0)
-            sort_odd(nc.scalar.copy, 3, 1)
             sort_even(nc.vector.tensor_copy, 2, 0, 1)
+            sort_odd(nc.scalar.copy, 3, 1)
             sort_odd(nc.vector.tensor_copy, 1, 0)
-            sort_even(nc.scalar.copy, 4, 1, 1)
+            sort_even(nc.vector.tensor_copy, 4, 1, 1)
+            for k in range(AHEAD):
+                transpose_tap(k)
+                empty_tap(k)
+            quantise_tap(0)
 
-            for k0 in range(0, TAPS, 2):
-                n_k = min(2, TAPS - k0)
-                grouped = stream.tile([P, 4096], BF16, name="grouped", bufs=3, align_bytes=64)
-                words = grouped[:].bitcast(F32).rearrange("r (k g b u) -> r k g b u", k=2, g=PASSES, u=2)
-                for k in range(k0, k0 + n_k):
-                    i, j = divmod(k, 3)
-                    for g0 in range(0, PASSES, 2):
-                        flipped = psum.tile([P, 2, 2, P], F32, name="flipped", tag="bank")
-                        for g in range(g0, g0 + 2):
-                            first = (8 * g + i) * ROW_WORDS
-                            for u in range(2):
-                                nc.tensor.transpose(
-                                    flipped[:, g - g0, u, :], pairs[:, j + 2 * u, first : first + P], identity[:]
-                                )
-                        nc.scalar.copy(
-                            out=words[:, k - k0, g0 : g0 + 2], in_=flipped[:].rearrange("r g u b -> r g b u")
-                        )
-                nc.vector.quantize_mx(
-                    out=u_codes[:, k0 : k0 + n_k].rearrange("r k g b -> r (k g b)").bitcast(FP8X4),
-                    scales=u_planes[:, k0 : k0 + n_k].rearrange("r k g b -> r (k g b)"),
-                    in_=grouped[:, 0 : n_k * 2048],
-                )
+            for step in range(STEPS + 12):
+                e, k = divmod(step, TAPS)
+                if step + AHEAD < TAPS:
+                    transpose_tap(step + AHEAD)
+                if step < STEPS:
+                    first_product(e, k)
+                if 1 <= step <= STEPS:
+                    empty_a(*divmod(step - 1, TAPS))
+                if step + 1 < TAPS:
+                    quantise_tap(step + 1)
+                if step + AHEAD < TAPS:
+                    empty_tap(step + AHEAD)
+                for e in range(GROUPS):
+                    for k0, n_k in A_RUNS:
+                        if step == e * TAPS + k0 + n_k + 2:
+                            quantise_a(e, k0, n_k)
+                    for k in range(TAPS):
+                        if step == p_step(e, k) and k not in VECTOR_TAPS:
+                            subtract(e, k)
+                    for k in range(TAPS):
+                        if step == p_step(e, k) + 1:
+                            regroup(e, k)
+                    for k0, n_k in P_RUNS:
+                        if step == p_step(e, k0 + n_k - 1) + 3:
+                            quantise_p(e, k0, n_k)
+                        a0, a_n = run_of(A_RUNS, k0 + n_k - 1)
+                        if step == max(p_step(e, k0 + n_k - 1) + 8, e * TAPS + a0 + a_n + 3):
+                            second_product(e, k0, n_k)
+                    if e == 0 and step == p_step(0, TAPS - 1) + 3:
+                        load_group(3)
 
-        late = ctx.enter_context(tc.tile_pool(name="late", bufs=1))
-        a_codes = late.tile([P, GROUPS * TAPS, P], U32, align_bytes=64)
-        a_planes = late.tile([P, GROUPS * TAPS, P], U8, align_bytes=64)
-
-        def first_product(e):
-            for k0, n_k in A_RUNS:
-                a_grouped = stream.tile([P, 4, P, PACK], BF16, name="a_grouped", align_bytes=64)
-                for k in range(k0, k0 + n_k):
-                    bank = psum.tile([P, PACK, P], F32, name="bank", tag="bank")
-                    for t in range(PACK):
-                        m0 = 512 * e + P * t
-                        c0 = m0 % (NEURONS // 2)
-                        for g in range(PASSES):
-                            nc.tensor.matmul_mx(
-                                out=bank[:, t, :],
-                                lhsT=g_codes[e // 2][:, g, c0 : c0 + P].bitcast(FP8X4),
-                                lhsT_scale=g_planes[4 * g : P, m0 : m0 + P],
-                                rhs=u_codes[:, k, g, :].bitcast(FP8X4),
-                                rhs_scale=u_planes[:, k, g, :],
-                                start=(g == 0),
-                                stop=(g == PASSES - 1),
-                            )
-                    nc.scalar.copy(out=a_grouped[:, k - k0], in_=bank[:].rearrange("r t b -> r b t"))
-                s0 = e * TAPS + k0
-                nc.vector.quantize_mx(
-                    out=a_codes[:, s0 : s0 + n_k].rearrange("r s b -> r (s b)").bitcast(FP8X4),
-                    scales=a_planes[:, s0 : s0 + n_k].rearrange("r s b -> r (s b)"),
-                    in_=a_grouped[:, 0:n_k].rearrange("r s b t -> r (s b t)"),
-                )
-
-        def regroup(copy, grouped, v_group, k0, first, n_k):
-            copy(
-                out=grouped[:, (first - k0) * 1024 : (first - k0 + n_k) * 1024].rearrange(
-                    "r (c i t) -> r c t i", i=4, t=PACK
-                ),
-                in_=v_group[:, :, first * OUTS : (first + n_k) * OUTS].rearrange("r t (c i) -> r c t i", i=4),
-            )
-
-        def difference(e):
-            v_group = v_groups[e]
-            for t in range(PACK):
-                nc.vector.tensor_tensor(
-                    out=v_group[:, t, :],
-                    in0=v_group[:, t, :],
-                    in1=w_groups[e][:, t, :],
-                    op=mybir.AluOpType.subtract,
-                )
-            for k0, n_k, n_scalar in P_RUNS:
-                grouped = stream.tile([P, 4096], BF16, name="grouped", bufs=3, align_bytes=64)
-                regroup(nc.scalar.copy, grouped, v_group, k0, k0, n_scalar)
-                if n_k > n_scalar:
-                    regroup(nc.vector.tensor_copy, grouped, v_group, k0, k0 + n_scalar, n_k - n_scalar)
-                s0 = e * TAPS + k0
-                nc.vector.quantize_mx(
-                    out=p_codes[:, s0 : s0 + n_k].rearrange("r s o -> r (s o)").bitcast(FP8X4),
-                    scales=p_planes[:, s0 : s0 + n_k].rearrange("r s o -> r (s o)"),
-                    in_=grouped[:, 0 : n_k * 1024],
-                )
-
-        def second_product(e):
-            for s in range(e * TAPS, (e + 1) * TAPS):
-                nc.tensor.matmul_mx(
-                    out=out_sum[:],
-                    lhsT=a_codes[:, s, :].bitcast(FP8X4),
-                    lhsT_scale=a_planes[:, s, :],
-                    rhs=p_codes[:, s, :].bitcast(FP8X4),
-                    rhs_scale=p_planes[:, s, :],
-                    start=(s == 0),
-                    stop=(s == GROUPS * TAPS - 1),
-                )
-
-        for e in range(GROUPS):
-            first_product(e)
-            difference(e)
-            if e + 2 < GROUPS:
-                load_group(e + 2)
-            if e > 0:
-                second_product(e - 1)
-        second_product(GROUPS - 1)
-
-        nc.vector.tensor_copy(out=result[:], in_=out_sum[:])
-        nc.sync.dma_start(out=out, in_=result[:])
+            nc.vector.tensor_copy(out=result[:], in_=out_sum[:])
+            nc.sync.dma_start(out=out, in_=result[:])

@@ -192,9 +192,7 @@ def tile_convexrelucnn_w_kernel(tc, x, G_words, G_scales, v, w, out):
             if k not in VECTOR_TAPS:
                 nc.scalar.copy(out=by_out(e, k), in_=by_plane(e, k, 0))
             else:
-                nc.vector.tensor_tensor(
-                    out=by_out(e, k), in0=by_plane(e, k, 0), in1=by_plane(e, k, 1), op=mybir.AluOpType.subtract
-                )
+                nc.vector.tensor_copy(out=by_out(e, k), in_=by_plane(e, k, 0))
 
         def quantise_p(e, k0, n_k):
             if k0 == 0:
@@ -268,7 +266,7 @@ def tile_convexrelucnn_w_kernel(tc, x, G_words, G_scales, v, w, out):
                         if step == e * TAPS + k0 + n_k + 2:
                             quantise_a(e, k0, n_k)
                     for k in range(TAPS):
-                        if step == p_step(e, k) and k not in VECTOR_TAPS:
+                        if step == p_step(e, k):
                             subtract(e, k)
                     for k in range(TAPS):
                         if step == p_step(e, k) + 1:

@@ -24,7 +24,7 @@ FLOPS = 2 * P * TAPS * NEURONS * 2048 + 2 * P * TAPS * NEURONS * OUTS
 
 A_RUNS = ((0, 4), (4, 4), (8, 1))
 P_RUNS = ((0, 2), (2, 2), (4, 2), (6, 2), (8, 1))
-VECTOR_TAPS = (1, 3, 5, 7)
+VECTOR_TAPS = (2, 5, 8)
 STEPS = GROUPS * TAPS
 AHEAD = 2
 

@@ -25,6 +25,7 @@ FLOPS = 2 * P * TAPS * NEURONS * 2048 + 2 * P * TAPS * NEURONS * OUTS
 A_RUNS = ((0, 4), (4, 4), (8, 1))
 P_RUNS = ((0, 2), (2, 2), (4, 2), (6, 2), (8, 1))
 VECTOR_TAPS = (2, 5, 8)
+LOAD_RUNS = ((0, 4), (4, 3), (7, 2))
 STEPS = GROUPS * TAPS
 AHEAD = 2
 
@@ -80,7 +81,7 @@ def tile_convexrelucnn_w_kernel(tc, x, G_words, G_scales, v, w, out):
                 parts[e, k] = (v_part, w_part, k - k0)
 
         def load_group(e):
-            for k0, n_k in ((0, 4), (4, 5)) if e in (0, 3) else ((0, TAPS),):
+            for k0, n_k in LOAD_RUNS:
                 load_taps(e, k0, n_k)
 
         def sort_even(copy, s, first_word, u):

@@ -25,13 +25,18 @@ FLOPS = 2 * P * TAPS * NEURONS * 2048 + 2 * P * TAPS * NEURONS * OUTS
 A_RUNS = ((0, 4), (4, 4), (8, 1))
 P_RUNS = ((0, 2), (2, 2), (4, 2), (6, 2), (8, 1))
 VECTOR_TAPS = (2, 5, 8)
-LOAD_RUNS = ((0, 4), (4, 3), (7, 2))
+LOAD_RUNS = (
+    ((0, 4), (4, 5)),
+    ((0, TAPS),),
+    ((0, 4), (4, 5)),
+    ((0, 4), (4, 3), (7, 2)),
+)
 STEPS = GROUPS * TAPS
 AHEAD = 2
 
 
 def p_step(e, k):
-    return 1 + (e * TAPS + k) * 1 // 1
+    return 2 + (e * TAPS + k) * 1 // 1
 
 
 def tile_convexrelucnn_w_kernel(tc, x, G_words, G_scales, v, w, out):
@@ -81,7 +86,7 @@ def tile_convexrelucnn_w_kernel(tc, x, G_words, G_scales, v, w, out):
                 parts[e, k] = (v_part, w_part, k - k0)
 
         def load_group(e):
-            for k0, n_k in LOAD_RUNS:
+            for k0, n_k in LOAD_RUNS[e]:
                 load_taps(e, k0, n_k)
 
         def sort_even(copy, s, first_word, u):

@@ -24,10 +24,10 @@ FLOPS = 2 * P * TAPS * NEURONS * 2048 + 2 * P * TAPS * NEURONS * OUTS
 
 A_RUNS = ((0, 4), (4, 4), (8, 1))
 P_RUNS = ((0, 2), (2, 2), (4, 2), (6, 2), (8, 1))
-VECTOR_TAPS = (2, 5, 8)
+VECTOR_TAPS = (1, 4, 7)
 LOAD_RUNS = (
     ((0, 4), (4, 5)),
-    ((0, TAPS),),
+    ((0, 4), (4, 5)),
     ((0, 4), (4, 5)),
     ((0, 4), (4, 3), (7, 2)),
 )
@@ -36,7 +36,7 @@ AHEAD = 2
 
 
 def p_step(e, k):
-    return 2 + (e * TAPS + k) * 1 // 1
+    return 3 + (e * TAPS + k) * 8 // 9
 
 
 def tile_convexrelucnn_w_kernel(tc, x, G_words, G_scales, v, w, out):
@@ -160,7 +160,7 @@ def tile_convexrelucnn_w_kernel(tc, x, G_words, G_scales, v, w, out):
         def empty_a(e, k):
             k0, n_k = run_of(A_RUNS, k)
             if k == k0:
-                a_runs[e, k0] = stream.tile([P, 4, P, PACK], BF16, name="a_grouped", bufs=3, align_bytes=64)
+                a_runs[e, k0] = stream.tile([P, 4, P, PACK], BF16, name="a_grouped", bufs=2, align_bytes=64)
             nc.scalar.copy(out=a_runs[e, k0][:, k - k0], in_=a_banks[e, k][:].rearrange("r t b -> r b t"))
 
         def quantise_a(e, k0, n_k):
@@ -257,8 +257,9 @@ def tile_convexrelucnn_w_kernel(tc, x, G_words, G_scales, v, w, out):
 
             for step in range(STEPS + 12):
                 e, k = divmod(step, TAPS)
-                if step + AHEAD < TAPS:
-                    transpose_tap(step + AHEAD)
+                if step % 2 == 0:
+                    for ahead in range(step + AHEAD, min(step + AHEAD + 2, TAPS)):
+                        transpose_tap(ahead)
                 if step < STEPS:
                     first_product(e, k)
                 if 1 <= step <= STEPS:
@@ -269,7 +270,7 @@ def tile_convexrelucnn_w_kernel(tc, x, G_words, G_scales, v, w, out):
                     empty_tap(step + AHEAD)
                 for e in range(GROUPS):
                     for k0, n_k in A_RUNS:
-                        if step == e * TAPS + k0 + n_k + 2:
+                        if step == e * TAPS + k0 + n_k + 1:
                             quantise_a(e, k0, n_k)
                     for k in range(TAPS):
                         if step == p_step(e, k):
@@ -281,7 +282,7 @@ def tile_convexrelucnn_w_kernel(tc, x, G_words, G_scales, v, w, out):
                         if step == p_step(e, k0 + n_k - 1) + 3:
                             quantise_p(e, k0, n_k)
                         a0, a_n = run_of(A_RUNS, k0 + n_k - 1)
-                        if step == max(p_step(e, k0 + n_k - 1) + 8, e * TAPS + a0 + a_n + 3):
+                        if step == max(p_step(e, k0 + n_k - 1) + 8, e * TAPS + a0 + a_n + 2):
                             second_product(e, k0, n_k)
                     if e == 0 and step == p_step(0, TAPS - 1) + 3:
                         load_group(3)

@@ -25,14 +25,9 @@ FLOPS = 2 * P * TAPS * NEURONS * 2048 + 2 * P * TAPS * NEURONS * OUTS
 A_RUNS = ((0, 4), (4, 4), (8, 1))
 P_RUNS = ((0, 2), (2, 2), (4, 2), (6, 2), (8, 1))
 VECTOR_TAPS = (1, 4, 7)
-LOAD_RUNS = (
-    ((0, 4), (4, 5)),
-    ((0, 4), (4, 5)),
-    ((0, 4), (4, 5)),
-    ((0, 4), (4, 3), (7, 2)),
-)
+X_RUNS = (slice(0, 16), slice(16, 34))
 STEPS = GROUPS * TAPS
-AHEAD = 2
+AHEAD = 3
 
 
 def p_step(e, k):
@@ -52,6 +47,7 @@ def tile_convexrelucnn_w_kernel(tc, x, G_words, G_scales, v, w, out):
         u_planes = keep.tile([P, TAPS, PASSES, P], U8, align_bytes=64)
         result = keep.tile([P, OUTS], F32)
         identity = keep.tile([P, P], F32)
+        zeros = keep.tile([P, OUTS], BF16)
         x_sb = stream.tile([P, ROWS * COLS], BF16, name="x_sb", tag="a_codes", align_bytes=64)
         pairs = stream.tile([P, 5, ROWS * ROW_WORDS], F32, name="pairs", tag="p_codes", align_bytes=64)
         out_sum = psum_out.tile([P, OUTS], F32)
@@ -71,35 +67,43 @@ def tile_convexrelucnn_w_kernel(tc, x, G_words, G_scales, v, w, out):
             )
             g_codes.append(codes)
 
-        def load_taps(e, k0, n_k):
-            v_part = keep.tile([P, PACK, n_k * OUTS], BF16, name="v_taps%d_%d" % (e % 3, k0), align_bytes=64)
-            w_part = keep.tile([P, PACK, n_k * OUTS], BF16, name="w_taps%d_%d" % (e % 3, k0), align_bytes=64)
-            for t in range(PACK):
-                m0 = 512 * e + P * t
-                nc.sync.dma_start(
-                    out=v_part[:, t, :], in_=v[m0 : m0 + P, k0 : k0 + n_k].rearrange("r k o -> r (k o)")
-                )
-                nc.sync.dma_start(
-                    out=w_part[:, t, :], in_=w[m0 : m0 + P, k0 : k0 + n_k].rearrange("r k o -> r (k o)")
-                )
-            for k in range(k0, k0 + n_k):
+        def load_taps(e, k0, runs):
+            n_taps = runs[-1][0] + runs[-1][1] - k0
+            v_part = stream.tile([P, PACK, n_taps * OUTS], BF16, name="v_taps%d" % k0, align_bytes=64)
+            w_part = stream.tile([P, PACK, n_taps * OUTS], BF16, name="w_taps%d" % k0, align_bytes=64)
+            for first, n_k in runs:
+                cols = slice((first - k0) * OUTS, (first - k0 + n_k) * OUTS)
+                for t in range(PACK):
+                    m0 = 512 * e + P * t
+                    for source, part in ((v, v_part), (w, w_part)):
+                        nc.sync.dma_start(
+                            out=part[:, t, cols],
+                            in_=source[m0 : m0 + P, first : first + n_k].rearrange("r k o -> r (k o)"),
+                        )
+            for k in range(k0, k0 + n_taps):
                 parts[e, k] = (v_part, w_part, k - k0)
 
-        def load_group(e):
-            for k0, n_k in LOAD_RUNS[e]:
-                load_taps(e, k0, n_k)
+        def load_front(e):
+            load_taps(e, 0, ((0, 4),))
 
-        def sort_even(copy, s, first_word, u):
+        def load_back(e):
+            load_taps(e, 4, ((4, 3), (7, 2)) if e == GROUPS - 1 else ((4, 5),))
+
+        def sort_even(copy, rows, s, first_word, u):
             copy(
-                out=pairs[:, s].rearrange("b (h c) -> b h c", c=ROW_WORDS),
-                in_=x_words[:, :, first_word : first_word + 32].rearrange("b h (c u) -> b u h c", u=2)[:, u],
+                out=pairs[:, s].rearrange("b (h c) -> b h c", c=ROW_WORDS)[:, rows],
+                in_=x_words[:, rows, first_word : first_word + 32].rearrange("b h (c u) -> b u h c", u=2)[:, u],
             )
 
-        def sort_odd(copy, s, u):
+        def sort_odd(copy, rows, s, u):
             copy(
-                out=pairs[:, s].bitcast(BF16).rearrange("b (h c e) -> b h c e", c=ROW_WORDS, e=2),
-                in_=odd[:, u],
+                out=pairs[:, s].bitcast(BF16).rearrange("b (h c e) -> b h c e", c=ROW_WORDS, e=2)[:, rows],
+                in_=odd[:, u, rows],
             )
+
+        def warm_up(n):
+            for i in range(n):
+                nc.tensor.matmul(out_sum[:], zeros[:, 0:P], zeros[:], start=True, stop=True)
 
         u_banks = {}
 
@@ -228,7 +232,13 @@ def tile_convexrelucnn_w_kernel(tc, x, G_words, G_scales, v, w, out):
                 )
 
         with tc.manual_schedule():
-            nc.sync.dma_start(out=x_sb[:], in_=x.rearrange("b c h w -> b (c h w)"))
+            for rows in X_RUNS:
+                nc.sync.dma_start(
+                    out=x_sb[:, rows.start * COLS : rows.stop * COLS],
+                    in_=x[:, :, rows].rearrange("b c h w -> b (c h w)"),
+                )
+            nc.vector.memset(zeros[:], 0.0)
+            warm_up(6)
             nc.vector.memset(g_planes[:].bitcast(I32), 0)
             for a in range(4):
                 nc.sync.dma_start(
@@ -236,22 +246,26 @@ def tile_convexrelucnn_w_kernel(tc, x, G_words, G_scales, v, w, out):
                     in_=G_scales[:, 4 * a : 4 * a + 4, :].bitcast(I32),
                 )
             make_identity(nc, identity[:])
-            for e in range(3):
+            for e in range(2):
                 load_g(e)
-                load_group(e)
-            load_g(3)
+                load_front(e)
+                load_back(e)
+            load_g(2)
 
             x_words = x_sb[:].bitcast(F32).rearrange("b (h c) -> b h c", c=COLS // 2)
             odd = x_sb[:].rearrange("b (h c) -> b h c", c=COLS)[:, :, 1:65].rearrange(
                 "b h (c u e) -> b u h c e", u=2, e=2
             )
-            sort_even(nc.vector.tensor_copy, 0, 0, 0)
-            sort_even(nc.vector.tensor_copy, 2, 0, 1)
-            sort_odd(nc.scalar.copy, 3, 1)
-            sort_odd(nc.vector.tensor_copy, 1, 0)
-            sort_even(nc.vector.tensor_copy, 4, 1, 1)
+            for rows in X_RUNS:
+                sort_even(nc.vector.tensor_copy, rows, 0, 0, 0)
+                sort_even(nc.vector.tensor_copy, rows, 2, 0, 1)
+                sort_odd(nc.scalar.copy, rows, 3, 1)
+            for rows in X_RUNS:
+                sort_odd(nc.vector.tensor_copy, rows, 1, 0)
+                sort_even(nc.vector.tensor_copy, rows, 4, 1, 1)
             for k in range(AHEAD):
                 transpose_tap(k)
+                warm_up(2)
                 empty_tap(k)
             quantise_tap(0)
 
@@ -279,13 +293,18 @@ def tile_convexrelucnn_w_kernel(tc, x, G_words, G_scales, v, w, out):
                         if step == p_step(e, k) + 1:
                             regroup(e, k)
                     for k0, n_k in P_RUNS:
-                        if step == p_step(e, k0 + n_k - 1) + 3:
+                        if step == p_step(e, k0 + n_k - 1) + (2 if e == GROUPS - 1 else 3):
                             quantise_p(e, k0, n_k)
                         a0, a_n = run_of(A_RUNS, k0 + n_k - 1)
                         if step == max(p_step(e, k0 + n_k - 1) + 8, e * TAPS + a0 + a_n + 2):
                             second_product(e, k0, n_k)
-                    if e == 0 and step == p_step(0, TAPS - 1) + 3:
-                        load_group(3)
+                    if e + 2 < GROUPS:
+                        if step == p_step(e, 3) + 1:
+                            if e == 1:
+                                load_g(3)
+                            load_front(e + 2)
+                        if step == p_step(e, TAPS - 1) + 1:
+                            load_back(e + 2)
 
             nc.vector.tensor_copy(out=result[:], in_=out_sum[:])
             nc.sync.dma_start(out=out, in_=result[:])

@@ -26,6 +26,7 @@ A_RUNS = ((0, 4), (4, 4), (8, 1))
 P_RUNS = ((0, 2), (2, 2), (4, 2), (6, 2), (8, 1))
 VECTOR_TAPS = (1, 4, 7)
 X_RUNS = (slice(0, 16), slice(16, 34))
+SHIFT = 32
 STEPS = GROUPS * TAPS
 AHEAD = 3
 
@@ -43,13 +44,14 @@ def tile_convexrelucnn_w_kernel(tc, x, G_words, G_scales, v, w, out):
         psum_out = ctx.enter_context(tc.psum_pool(name="psum_out", bufs=1))
 
         g_planes = keep.tile([P, NEURONS], U8, align_bytes=64)
-        u_codes = keep.tile([P, TAPS, PASSES, P], U32, align_bytes=64)
+        u_block = keep.tile([P, SHIFT + TAPS * PASSES * P], U32, align_bytes=256)
+        u_codes = u_block[:, SHIFT:].rearrange("r (k g b) -> r k g b", k=TAPS, g=PASSES)
         u_planes = keep.tile([P, TAPS, PASSES, P], U8, align_bytes=64)
         result = keep.tile([P, OUTS], F32)
         identity = keep.tile([P, P], F32)
         zeros = keep.tile([P, OUTS], BF16)
-        x_sb = stream.tile([P, ROWS * COLS], BF16, name="x_sb", tag="a_codes", align_bytes=64)
-        pairs = stream.tile([P, 5, ROWS * ROW_WORDS], F32, name="pairs", tag="p_codes", align_bytes=64)
+        x_sb = stream.tile([P, ROWS * COLS], BF16, name="x_sb", tag="a_codes", align_bytes=256)
+        pairs = stream.tile([P, 5, ROWS * ROW_WORDS], F32, name="pairs", tag="p_codes", align_bytes=256)
         out_sum = psum_out.tile([P, OUTS], F32)
 
         g_codes = []
@@ -60,7 +62,7 @@ def tile_convexrelucnn_w_kernel(tc, x, G_words, G_scales, v, w, out):
         p_runs = {}
 
         def load_g(e):
-            codes = keep.tile([P, PASSES, 512], U32, name="g_codes%d" % e, align_bytes=64)
+            codes = keep.tile([P, PASSES, 512], U32, name="g_codes%d" % e, align_bytes=256)
             nc.sync.dma_start(
                 out=codes[:].bitcast(I32),
                 in_=G_words.rearrange("g r m t -> r g (m t)")[:, :, e * 2048 : (e + 1) * 2048].bitcast(I32),
@@ -169,8 +171,9 @@ def tile_convexrelucnn_w_kernel(tc, x, G_words, G_scales, v, w, out):
 
         def quantise_a(e, k0, n_k):
             if k0 == 0:
+                a_block = stream.tile([P, SHIFT + TAPS * P], U32, name="a_block", tag="a_codes", align_bytes=256)
                 a_groups[e] = (
-                    stream.tile([P, TAPS, P], U32, name="a_codes", align_bytes=64),
+                    a_block[:, SHIFT:].rearrange("r (k b) -> r k b", k=TAPS),
                     stream.tile([P, TAPS, P], U8, name="a_planes", align_bytes=64),
                 )
             a_codes, a_planes = a_groups[e]
@@ -207,7 +210,7 @@ def tile_convexrelucnn_w_kernel(tc, x, G_words, G_scales, v, w, out):
         def quantise_p(e, k0, n_k):
             if k0 == 0:
                 p_groups[e] = (
-                    stream.tile([P, TAPS, OUTS], U32, name="p_codes", align_bytes=64),
+                    stream.tile([P, TAPS, OUTS], U32, name="p_codes", align_bytes=256),
                     stream.tile([P, TAPS, OUTS], U8, name="p_planes", align_bytes=64),
                 )
             p_codes, p_planes = p_groups[e]

from contextlib import ExitStack

import concourse.mybir as mybir
from concourse.masks import make_identity

F32 = mybir.dt.float32
BF16 = mybir.dt.bfloat16
I32 = mybir.dt.int32
U32 = mybir.dt.uint32
U8 = mybir.dt.uint8
FP8X4 = mybir.dt.float8_e4m3fn_x4

P = 128
ROWS = 34
COLS = 66
TAPS = 9
NEURONS = 2048
OUTS = 256
PASSES = 4
GROUPS = 4
PACK = 4
ROW_WORDS = 16
FLOPS = 2 * P * TAPS * NEURONS * 2048 + 2 * P * TAPS * NEURONS * OUTS

A_RUNS = ((0, 4), (4, 4), (8, 1))
P_RUNS = ((0, 2), (2, 2), (4, 2), (6, 2), (8, 1))
VECTOR_TAPS = (1, 4, 7)
X_RUNS = (slice(0, 16), slice(16, 34))
SHIFT = 32
STEPS = GROUPS * TAPS
AHEAD = 3


def p_step(e, k):
    return 3 + (e * TAPS + k) * 8 // 9


def tile_convexrelucnn_w_kernel(tc, x, G_words, G_scales, v, w, out):
    nc = tc.nc
    with ExitStack() as ctx:
        keep = ctx.enter_context(tc.tile_pool(name="keep", bufs=1))
        stream = ctx.enter_context(tc.tile_pool(name="stream", bufs=2))
        psum = ctx.enter_context(tc.psum_pool(name="psum", bufs=7))
        psum_out = ctx.enter_context(tc.psum_pool(name="psum_out", bufs=1))

        g_planes = keep.tile([P, NEURONS], U8, align_bytes=64)
        u_block = keep.tile([P, SHIFT + TAPS * PASSES * P], U32, align_bytes=256)
        u_codes = u_block[:, SHIFT:].rearrange("r (k g b) -> r k g b", k=TAPS, g=PASSES)
        u_planes = keep.tile([P, TAPS, PASSES, P], U8, align_bytes=64)
        result = keep.tile([P, OUTS], F32)
        identity = keep.tile([P, P], F32)
        zeros = keep.tile([P, OUTS], BF16)
        x_sb = stream.tile([P, ROWS * COLS], BF16, name="x_sb", tag="a_codes", align_bytes=256)
        pairs = stream.tile([P, 5, ROWS * ROW_WORDS], F32, name="pairs", tag="p_codes", align_bytes=256)
        out_sum = psum_out.tile([P, OUTS], F32)

        g_codes = []
        parts = {}
        a_groups = {}
        p_groups = {}
        a_runs = {}
        p_runs = {}

        def load_g(e):
            codes = keep.tile([P, PASSES, 512], U32, name="g_codes%d" % e, align_bytes=256)
            nc.sync.dma_start(
                out=codes[:].bitcast(I32),
                in_=G_words.rearrange("g r m t -> r g (m t)")[:, :, e * 2048 : (e + 1) * 2048].bitcast(I32),
            )
            g_codes.append(codes)

        def load_taps(e, k0, runs):
            n_taps = runs[-1][0] + runs[-1][1] - k0
            v_part = stream.tile([P, PACK, n_taps * OUTS], BF16, name="v_taps%d" % k0, align_bytes=64)
            w_part = stream.tile([P, PACK, n_taps * OUTS], BF16, name="w_taps%d" % k0, align_bytes=64)
            for first, n_k in runs:
                cols = slice((first - k0) * OUTS, (first - k0 + n_k) * OUTS)
                for t in range(PACK):
                    m0 = 512 * e + P * t
                    for source, part in ((v, v_part), (w, w_part)):
                        nc.sync.dma_start(
                            out=part[:, t, cols],
                            in_=source[m0 : m0 + P, first : first + n_k].rearrange("r k o -> r (k o)"),
                        )
            for k in range(k0, k0 + n_taps):
                parts[e, k] = (v_part, w_part, k - k0)

        def load_front(e):
            load_taps(e, 0, ((0, 4),))

        def load_back(e):
            load_taps(e, 4, ((4, 3), (7, 2)) if e == GROUPS - 1 else ((4, 5),))

        def sort_even(copy, rows, s, first_word, u):
            copy(
                out=pairs[:, s].rearrange("b (h c) -> b h c", c=ROW_WORDS)[:, rows],
                in_=x_words[:, rows, first_word : first_word + 32].rearrange("b h (c u) -> b u h c", u=2)[:, u],
            )

        def sort_odd(copy, rows, s, u):
            copy(
                out=pairs[:, s].bitcast(BF16).rearrange("b (h c e) -> b h c e", c=ROW_WORDS, e=2)[:, rows],
                in_=odd[:, u, rows],
            )

        def warm_up(n):
            for i in range(n):
                nc.tensor.matmul(out_sum[:], zeros[:, 0:P], zeros[:], start=True, stop=True)

        u_banks = {}

        def transpose_tap(k):
            i, j = divmod(k, 3)
            banks = []
            for g0 in range(0, PASSES, 2):
                flipped = psum.tile([P, 2, 2, P], F32, name="flipped", tag="bank")
                for g in range(g0, g0 + 2):
                    first = (8 * g + i) * ROW_WORDS
                    for u in range(2):
                        nc.tensor.transpose(
                            flipped[:, g - g0, u, :], pairs[:, j + 2 * u, first : first + P], identity[:]
                        )
                banks.append(flipped)
            u_banks[k] = banks

        u_grouped = {}

        def empty_tap(k):
            grouped = stream.tile([P, 2048], BF16, name="grouped", bufs=4, align_bytes=64)
            words = grouped[:, 0:2048].bitcast(F32).rearrange("r (g b u) -> r g b u", g=PASSES, u=2)
            for half, copy in enumerate((nc.scalar.copy, nc.vector.tensor_copy)):
                copy(
                    out=words[:, 2 * half : 2 * half + 2],
                    in_=u_banks[k][half][:].rearrange("r g u b -> r g b u"),
                )
            u_grouped[k] = grouped

        def quantise_tap(k):
            nc.vector.quantize_mx(
                out=u_codes[:, k].rearrange("r g b -> r (g b)").bitcast(FP8X4),
                scales=u_planes[:, k].rearrange("r g b -> r (g b)"),
                in_=u_grouped[k][:, 0:2048],
            )

        a_banks = {}

        def first_product(e, k):
            bank = psum.tile([P, PACK, P], F32, name="bank", tag="bank")
            for t in range(PACK):
                m0 = 512 * e + P * t
                for g in range(PASSES):
                    nc.tensor.matmul_mx(
                        out=bank[:, t, :],
                        lhsT=g_codes[e][:, g, P * t : P * t + P].bitcast(FP8X4),
                        lhsT_scale=g_planes[4 * g : P, m0 : m0 + P],
                        rhs=u_codes[:, k, g, :].bitcast(FP8X4),
                        rhs_scale=u_planes[:, k, g, :],
                        start=(g == 0),
                        stop=(g == PASSES - 1),
                    )
            a_banks[e, k] = bank

        def run_of(runs, k):
            return [run for run in runs if run[0] <= k < run[0] + run[1]][0]

        def empty_a(e, k):
            k0, n_k = run_of(A_RUNS, k)
            if k == k0:
                a_runs[e, k0] = stream.tile([P, 4, P, PACK], BF16, name="a_grouped", bufs=2, align_bytes=64)
            nc.scalar.copy(out=a_runs[e, k0][:, k - k0], in_=a_banks[e, k][:].rearrange("r t b -> r b t"))

        def quantise_a(e, k0, n_k):
            if k0 == 0:
                a_block = stream.tile([P, SHIFT + TAPS * P], U32, name="a_block", tag="a_codes", align_bytes=256)
                a_groups[e] = (
                    a_block[:, SHIFT:].rearrange("r (k b) -> r k b", k=TAPS),
                    stream.tile([P, TAPS, P], U8, name="a_planes", align_bytes=64),
                )
            a_codes, a_planes = a_groups[e]
            nc.vector.quantize_mx(
                out=a_codes[:, k0 : k0 + n_k].rearrange("r s b -> r (s b)").bitcast(FP8X4),
                scales=a_planes[:, k0 : k0 + n_k].rearrange("r s b -> r (s b)"),
                in_=a_runs[e, k0][:, 0:n_k].rearrange("r s b t -> r (s b t)"),
            )

        def subtract(e, k):
            v_part, w_part, at = parts[e, k]
            cols = slice(at * OUTS, (at + 1) * OUTS)
            nc.vector.tensor_tensor(
                out=v_part[:, :, cols], in0=v_part[:, :, cols], in1=w_part[:, :, cols], op=mybir.AluOpType.subtract
            )

        def by_plane(e, k, which):
            part = parts[e, k][which]
            at = parts[e, k][2] * OUTS
            return part[:, :, at : at + OUTS].rearrange("r t (c i) -> r c t i", i=4)

        def by_out(e, k):
            k0, n_k = run_of(P_RUNS, k)
            if (e, k0) not in p_runs:
                p_runs[e, k0] = stream.tile([P, 2048], BF16, name="grouped", bufs=4, align_bytes=64)
            return p_runs[e, k0][:, (k - k0) * 1024 : (k - k0 + 1) * 1024].rearrange("r (c i t) -> r c t i", i=4, t=PACK)

        def regroup(e, k):
            if k not in VECTOR_TAPS:
                nc.scalar.copy(out=by_out(e, k), in_=by_plane(e, k, 0))
            else:
                nc.vector.tensor_copy(out=by_out(e, k), in_=by_plane(e, k, 0))

        def quantise_p(e, k0, n_k):
            if k0 == 0:
                p_groups[e] = (
                    stream.tile([P, TAPS, OUTS], U32, name="p_codes", align_bytes=256),
                    stream.tile([P, TAPS, OUTS], U8, name="p_planes", align_bytes=64),
                )
            p_codes, p_planes = p_groups[e]
            nc.vector.quantize_mx(
                out=p_codes[:, k0 : k0 + n_k].rearrange("r s o -> r (s o)").bitcast(FP8X4),
                scales=p_planes[:, k0 : k0 + n_k].rearrange("r s o -> r (s o)"),
                in_=p_runs[e, k0][:, 0 : n_k * 1024],
            )

        def second_product(e, k0, n_k):
            a_codes, a_planes = a_groups[e]
            p_codes, p_planes = p_groups[e]
            for k in range(k0, k0 + n_k):
                nc.tensor.matmul_mx(
                    out=out_sum[:],
                    lhsT=a_codes[:, k, :].bitcast(FP8X4),
                    lhsT_scale=a_planes[:, k, :],
                    rhs=p_codes[:, k, :].bitcast(FP8X4),
                    rhs_scale=p_planes[:, k, :],
                    start=(e == 0 and k == 0),
                    stop=(e == GROUPS - 1 and k == TAPS - 1),
                )

        with tc.manual_schedule():
            for rows in X_RUNS:
                nc.sync.dma_start(
                    out=x_sb[:, rows.start * COLS : rows.stop * COLS],
                    in_=x[:, :, rows].rearrange("b c h w -> b (c h w)"),
                )
            nc.vector.memset(zeros[:], 0.0)
            warm_up(6)
            nc.vector.memset(g_planes[:].bitcast(I32), 0)
            for a in range(4):
                nc.sync.dma_start(
                    out=g_planes[32 * a : 32 * a + 16, :].bitcast(I32),
                    in_=G_scales[:, 4 * a : 4 * a + 4, :].bitcast(I32),
                )
            make_identity(nc, identity[:])
            for e in range(2):
                load_g(e)
                load_front(e)
                load_back(e)
            load_g(2)

            x_words = x_sb[:].bitcast(F32).rearrange("b (h c) -> b h c", c=COLS // 2)
            odd = x_sb[:].rearrange("b (h c) -> b h c", c=COLS)[:, :, 1:65].rearrange(
                "b h (c u e) -> b u h c e", u=2, e=2
            )
            for rows in X_RUNS:
                sort_even(nc.vector.tensor_copy, rows, 0, 0, 0)
                sort_even(nc.vector.tensor_copy, rows, 2, 0, 1)
                sort_odd(nc.scalar.copy, rows, 3, 1)
            for rows in X_RUNS:
                sort_odd(nc.vector.tensor_copy, rows, 1, 0)
                sort_even(nc.vector.tensor_copy, rows, 4, 1, 1)
            for k in range(AHEAD):
                transpose_tap(k)
                warm_up(2)
                empty_tap(k)
            quantise_tap(0)

            for step in range(STEPS + 12):
                e, k = divmod(step, TAPS)
                if step % 2 == 0:
                    for ahead in range(step + AHEAD, min(step + AHEAD + 2, TAPS)):
                        transpose_tap(ahead)
                if step < STEPS:
                    first_product(e, k)
                if 1 <= step <= STEPS:
                    empty_a(*divmod(step - 1, TAPS))
                if step + 1 < TAPS:
                    quantise_tap(step + 1)
                if step + AHEAD < TAPS:
                    empty_tap(step + AHEAD)
                for e in range(GROUPS):
                    for k0, n_k in A_RUNS:
                        if step == e * TAPS + k0 + n_k + 1:
                            quantise_a(e, k0, n_k)
                    for k in range(TAPS):
                        if step == p_step(e, k):
                            subtract(e, k)
                    for k in range(TAPS):
                        if step == p_step(e, k) + 1:
                            regroup(e, k)
                    for k0, n_k in P_RUNS:
                        if step == p_step(e, k0 + n_k - 1) + (2 if e == GROUPS - 1 else 3):
                            quantise_p(e, k0, n_k)
                        a0, a_n = run_of(A_RUNS, k0 + n_k - 1)
                        if step == max(p_step(e, k0 + n_k - 1) + 8, e * TAPS + a0 + a_n + 2):
                            second_product(e, k0, n_k)
                    if e + 2 < GROUPS:
                        if step == p_step(e, 3) + 1:
                            if e == 1:
                                load_g(3)
                            load_front(e + 2)
                        if step == p_step(e, TAPS - 1) + 1:
                            load_back(e + 2)

            nc.vector.tensor_copy(out=result[:], in_=out_sum[:])
            nc.sync.dma_start(out=out, in_=result[:])
